import numpy as np
import ml_dtypes


def mxq(x, axis, fmt="e4m3"):
    dtype, down = {"e4m3": (ml_dtypes.float8_e4m3fn, 7), "e5m2": (ml_dtypes.float8_e5m2, 14)}[fmt]
    v = np.moveaxis(np.asarray(x, np.float32).astype(ml_dtypes.bfloat16).astype(np.float64), axis, -1)
    blocks = v.reshape(v.shape[:-1] + (-1, 32))
    amax = np.abs(blocks).max(-1, keepdims=True)
    byte = np.maximum(np.where(amax > 0, np.frexp(amax)[1] - 1 + 127, 0) - down, 1)
    scale = np.exp2(byte - 127.0)
    codes = (blocks / scale).astype(np.float32).astype(dtype).astype(np.float64)
    return np.moveaxis((codes * scale).reshape(v.shape), -1, axis)


WIDE = False


def mx_kscale(k):
    if not WIDE:
        return np.ones(k)
    levels = np.array([10, -10, 5, -5, 0])
    if k % 512:
        return np.exp2(np.random.permutation(np.resize(levels, k // 32))).repeat(32)
    a = np.empty((k // 512, 16))
    for p in range(k // 512):
        a[p, :8] = np.random.permutation(np.resize(levels, 8))
        for g in range(8):
            far = levels[np.abs(levels - a[p, g]) >= 10]
            a[p, g + 8] = far[np.random.randint(len(far))]
    return np.exp2(a.ravel()).repeat(32)


BF16 = ml_dtypes.bfloat16


def bf(x):
    return np.asarray(x, np.float32).astype(BF16)


def f64(x):
    return np.asarray(x).astype(np.float64)


N, IN_F, J, K = 256, 2048, 128, 16


def setup_inputs():
    s = mx_kscale(IN_F)
    s = s / s.max()
    return {"tensor": bf(np.random.standard_normal((N, IN_F)) * s),
            "T": bf(np.random.standard_normal((IN_F, J, K)) * 4.0 / (K * np.sqrt(IN_F)) / s[:, None, None])}


def core(tensor, T):
    x = f64(tensor).reshape(tensor.shape[0], -1)
    feats = (mxq(x, 1, "e4m3") @ mxq(f64(T).reshape(IN_F, J * K), 0, "e4m3")).reshape(N, J, K)
    diversity = np.stack([np.exp(-np.abs(feats[n][None, :, :] - feats).sum(axis=2)).sum(axis=0) for n in range(N)])
    return np.concatenate((x, diversity), axis=1)


def e4m3fn_bytes(y):
    return np.clip(np.asarray(y, np.float64), -448.0, 448.0).astype(np.float32).astype(ml_dtypes.float8_e4m3fn).view(np.uint8)


Y_SCALE = 110.0


def reference(tensor, T):
    out = core(tensor, T)
    return out, e4m3fn_bytes(out * Y_SCALE)

@@ -1,0 +1,268 @@
+from contextlib import ExitStack
+
+import concourse.mybir as mybir
+from concourse.masks import make_identity
+
+N, IN_F, J, K = 256, 2048, 128, 16
+Y_SCALE = 110.0
+FLOPS = 2 * N * IN_F * J * K + 3 * N * N * J * K
+
+F32 = mybir.dt.float32
+BF16 = mybir.dt.bfloat16
+U32 = mybir.dt.uint32
+U8 = mybir.dt.uint8
+FP8X4 = mybir.dt.float8_e4m3fn_x4
+FP8 = mybir.dt.float8_e4m3fn
+ALU = mybir.AluOpType
+ACT = mybir.ActivationFunctionType
+
+P = 128
+PASSES = 4
+NV = 120
+RV = 8
+RG = 4
+KV = 10
+LG = N - 1 - NV
+
+
+def tile_minibatchdiscriminator_kernel(tc, tensor, T, out_0, out_1):
+    nc = tc.nc
+    with ExitStack() as ctx:
+        cst = ctx.enter_context(tc.tile_pool(name="cst", bufs=1))
+        psum = ctx.enter_context(tc.psum_pool(name="psum", bufs=1))
+
+        ident = cst.tile([P, P], F32, name="ident")
+        rowsum = cst.tile([P, N], F32, name="rowsum")
+        colsum = cst.tile([P, N], F32, name="colsum")
+        sneg = cst.tile([P, N], F32, name="sneg")
+        ssum = cst.tile([P, N], F32, name="ssum")
+        fs = cst.tile([P, K, N], F32, name="fs")
+        ev = [cst.tile([P, RV, N], F32, name="ev%d" % i) for i in range(3)]
+        eg = [cst.tile([P, RG, LG], F32, name="eg%d" % i) for i in range(2)]
+        xs = [cst.tile([P, IN_F], BF16, name="xs%d" % t) for t in range(2)]
+
+        for t in range(2):
+            nc.sync.dma_start(out=xs[t][:], in_=tensor[t * P:(t + 1) * P, :])
+
+        make_identity(nc, ident[:])
+        nc.gpsimd.memset(rowsum[:], 0.0)
+        nc.gpsimd.memset(colsum[:], 0.0)
+        for e in ev:
+            nc.gpsimd.memset(e[:, :, 0:RV], 0.0)
+        for e in eg:
+            nc.gpsimd.memset(e[:, :, 0:RG], 0.0)
+
+        fp = []
+        with ExitStack() as pre:
+            rawp = pre.enter_context(tc.tile_pool(name="rawp", bufs=4))
+            grpp = pre.enter_context(tc.tile_pool(name="grpp", bufs=2))
+            keep = pre.enter_context(tc.tile_pool(name="keep", bufs=1))
+            tq = keep.tile([P, PASSES, J * K], U32, name="tq", align_bytes=64)
+            tsc = keep.tile([P, PASSES, J * K], U8, name="tsc", align_bytes=64)
+            xg = keep.tile([P, PASSES, N, 4], BF16, name="xg", align_bytes=64)
+            xq = keep.tile([P, PASSES * N], U32, name="xq", align_bytes=64)
+            xsc = keep.tile([P, PASSES * N], U8, name="xsc", align_bytes=64)
+
+            tv = T.rearrange("(s p t) j k -> s p t (j k)", p=P, t=4)
+            raws = []
+            for s in range(PASSES):
+                for h in range(2):
+                    raw = rawp.tile([P, 4, 1024], BF16, name="raw", tag="raw")
+                    nc.sync.dma_start(out=raw[:], in_=tv[s][:, :, h * 1024:(h + 1) * 1024])
+                    raws.append(raw)
+
+            for g in range(PASSES):
+                xt = psum.tile([P, 2, N], F32, name="xt", tag="b%d" % g)
+                for t in range(2):
+                    words = xs[t][:].bitcast(F32)
+                    for u in range(2):
+                        nc.tensor.transpose(xt[:, u, t * P:(t + 1) * P], words[:, 256 * g + u:256 * (g + 1):2], ident[:])
+                nc.vector.tensor_copy(out=xg[:, g, :, :].bitcast(F32), in_=xt[:].rearrange("p u n -> p n u"))
+            nc.vector.quantize_mx(out=xq[:].bitcast(FP8X4), scales=xsc[:], in_=xg[:].rearrange("p g n f -> p (g n f)"))
+
+            for b in range(8):
+                fpb = psum.tile([P, 2, N], F32, name="fp", tag="b%d" % b)
+                fp.append(fpb)
+
+            def mm(k, s):
+                nc.tensor.matmul_mx(
+                    out=fp[k // 2][:, k % 2, :],
+                    lhsT=tq[:, s, k * J:(k + 1) * J].bitcast(FP8X4),
+                    lhsT_scale=tsc[:, s, k * J:(k + 1) * J],
+                    rhs=xq[:, s * N:(s + 1) * N].bitcast(FP8X4),
+                    rhs_scale=xsc[:, s * N:(s + 1) * N],
+                    start=(s == 0),
+                    stop=(s == PASSES - 1),
+                )
+
+            for s in range(PASSES):
+                grp = grpp.tile([P, K, J, 4], BF16, name="grp", tag="grp", align_bytes=64)
+                for h in range(2):
+                    src = raws[2 * s + h][:].rearrange("p t (j k) -> p k j t", k=K)
+                    js = slice(64 * h, 64 * h + 64)
+                    nc.vector.tensor_copy(out=grp[:, 0:KV, js, :], in_=src[:, 0:KV, :, :])
+                    nc.scalar.copy(out=grp[:, KV:K, js, :], in_=src[:, KV:K, :, :])
+                for q in range(2):
+                    nc.vector.quantize_mx(
+                        out=tq[:, s, 1024 * q:1024 * (q + 1)].bitcast(FP8X4),
+                        scales=tsc[:, s, 1024 * q:1024 * (q + 1)],
+                        in_=grp[:, 8 * q:8 * (q + 1), :, :].rearrange("p k j t -> p (k j t)"),
+                    )
+                if s < PASSES - 1:
+                    for b in range(8):
+                        mm(2 * b, s)
+            for b in range(8):
+                mm(2 * b, PASSES - 1)
+                for s in range(PASSES):
+                    mm(2 * b + 1, s)
+
+        for b in range(8):
+            nc.scalar.copy(out=fs[:, 2 * b:2 * b + 2, :], in_=fp[b][:])
+            for kk in range(2):
+                for hf in range(2):
+                    cs = slice(hf * P, (hf + 1) * P)
+                    if b == 0 and kk == 0:
+                        nc.vector.tensor_scalar(out=sneg[:, cs], in0=fp[b][:, kk, cs], scalar1=-0.5, scalar2=None, op0=ALU.mult)
+                    else:
+                        nc.vector.scalar_tensor_tensor(out=sneg[:, cs], in0=fp[b][:, kk, cs], scalar=-0.5, in1=sneg[:, cs], op0=ALU.mult, op1=ALU.add)
+        nc.scalar.activation(out=ssum[:], in_=sneg[:], func=ACT.Copy, scale=-2.0)
+
+        with ExitStack() as mainctx:
+            apool = mainctx.enter_context(tc.tile_pool(name="apool", bufs=3))
+            accp = mainctx.enter_context(tc.tile_pool(name="accp", bufs=3))
+            xop = mainctx.enter_context(tc.tile_pool(name="xop", bufs=2))
+
+            vgroups = list(range(0, NV, RV))
+            ggroups = list(range(NV, N, RG))
+            accs = {}
+            atiles = {}
+
+            def vs(i):
+                n0 = vgroups[i]
+                lg = N - 1 - n0
+                acc = accp.tile([P, RV, N], F32, name="acc", tag="acc")
+                accs[i] = acc
+                for k in range(K):
+                    for r in range(RV):
+                        n = n0 + r
+                        nc.vector.scalar_tensor_tensor(
+                            out=acc[:, r, r:lg],
+                            in0=fp[k // 2][:, k % 2, n + 1:N],
+                            scalar=fs[:, k, n:n + 1],
+                            in1=(sneg[:, n + 1:N] if k == 0 else acc[:, r, r:lg]),
+                            op0=ALU.max,
+                            op1=ALU.add,
+                        )
+
+            def ve(i):
+                n0 = vgroups[i]
+                lg = N - 1 - n0
+                for r in range(RV):
+                    n = n0 + r
+                    nc.scalar.activation(out=ev[i % 3][:, r, r:lg], in_=accs[i][:, r, r:lg], func=ACT.Exp, scale=-2.0,
+                                         bias=ssum[:, n:n + 1], accum_out=rowsum[:, n:n + 1])
+
+            def fold(e, rows, n0):
+                lg = N - 1 - n0
+                h = rows // 2
+                while h >= 1:
+                    nc.gpsimd.tensor_tensor(out=e[:, 0:h, 0:lg], in0=e[:, 0:h, 0:lg], in1=e[:, h:2 * h, 0:lg], op=ALU.add)
+                    h = h // 2
+                nc.gpsimd.tensor_tensor(out=colsum[:, n0 + 1:N], in0=colsum[:, n0 + 1:N], in1=e[:, 0, 0:lg], op=ALU.add)
+
+            def ga(g):
+                n0 = ggroups[g]
+                lg = N - 1 - n0
+                a = apool.tile([P, K, RG, LG], F32, name="a", tag="a")
+                atiles[g] = a
+                for r in range(RG):
+                    for k in range(K):
+                        nc.scalar.activation(out=a[:, k, r, 0:lg], in_=fs[:, k, n0 + 1:N], func=ACT.Abs, scale=-1.0,
+                                             bias=fs[:, k, n0 + r:n0 + r + 1])
+
+            def gt(g):
+                n0 = ggroups[g]
+                lg = N - 1 - n0
+                a = atiles[g]
+                h = K // 2
+                while h >= 1:
+                    nc.gpsimd.tensor_tensor(out=a[:, 0:h, :, 0:lg], in0=a[:, 0:h, :, 0:lg], in1=a[:, h:2 * h, :, 0:lg], op=ALU.add)
+                    h = h // 2
+
+            def ge(g):
+                n0 = ggroups[g]
+                lg = N - 1 - n0
+                for r in range(RG):
+                    if r < lg:
+                        n = n0 + r
+                        nc.scalar.activation(out=eg[g % 2][:, r, r:lg], in_=atiles[g][:, 0, r, r:lg], func=ACT.Exp, scale=-1.0,
+                                             accum_out=rowsum[:, n:n + 1])
+
+            def xout(t):
+                xf = xop.tile([P, IN_F], F32, name="xf", tag="xf")
+                x8 = xop.tile([P, IN_F], FP8, name="x8", tag="x8")
+                nc.scalar.copy(out=xf[:], in_=xs[t][:])
+                nc.sync.dma_start(out=out_0[t * P:(t + 1) * P, 0:IN_F], in_=xf[:])
+                nc.scalar.activation(out=x8[:], in_=xf[:], func=ACT.Copy, scale=Y_SCALE, saturate=False)
+                nc.sync.dma_start(out=out_1[t * P:(t + 1) * P, 0:IN_F], in_=x8[:].bitcast(U8))
+
+            def cost_v(i):
+                return sum(K * (N - 1 - vgroups[i] - r + 18) for r in range(RV))
+
+            def cost_g(g):
+                return 2 * (K + 1) * RG * (N - 1 - ggroups[g]) + 1200
+
+            ng = len(ggroups)
+            nvg = len(vgroups)
+            ga(0)
+            ga(1)
+            clock_g = 0
+            clock_v = 0
+            iv = 0
+            done_at = []
+            next_ve = 0
+            for g in range(ng):
+                if g >= 1:
+                    ge(g - 1)
+                first_ve = next_ve
+                while next_ve < iv and done_at[next_ve] <= clock_g:
+                    ve(next_ve)
+                    next_ve += 1
+                while iv < nvg and clock_v <= clock_g + cost_g(g) and iv - next_ve < 3:
+                    vs(iv)
+                    clock_v += cost_v(iv)
+                    done_at.append(clock_v)
+                    iv += 1
+                if g + 2 < ng:
+                    ga(g + 2)
+                if g in (2, 4):
+                    xout(g // 2 - 1)
+                gt(g)
+                clock_g += cost_g(g)
+                if g >= 1:
+                    fold(eg[(g - 1) % 2], RG, ggroups[g - 1])
+                for i in range(first_ve, next_ve):
+                    fold(ev[i % 3], RV, vgroups[i])
+                    clock_g += 2 * RV * (N - 1 - vgroups[i])
+            ge(ng - 1)
+            fold(eg[(ng - 1) % 2], RG, ggroups[ng - 1])
+            while next_ve < nvg:
+                if iv < nvg and iv - next_ve < 2:
+                    vs(iv)
+                    iv += 1
+                else:
+                    ve(next_ve)
+                    fold(ev[next_ve % 3], RV, vgroups[next_ve])
+                    next_ve += 1
+
+            o0 = xop.tile([P, 2, J], F32, name="o0", tag="o0")
+            o8 = xop.tile([P, 2, J], FP8, name="o8", tag="o8")
+            pt = psum.tile([P, 2, J], F32, name="pt", tag="b0")
+            for t in range(2):
+                nc.tensor.matmul(out=pt[:, t, :], lhsT=rowsum[:, t * P:(t + 1) * P], rhs=ident[:], is_transpose=True, start=True, stop=False)
+                nc.tensor.matmul(out=pt[:, t, :], lhsT=colsum[:, t * P:(t + 1) * P], rhs=ident[:], is_transpose=True, start=False, stop=True)
+            nc.vector.tensor_scalar(out=o0[:], in0=pt[:], scalar1=1.0, scalar2=None, op0=ALU.add)
+            nc.scalar.activation(out=o8[:], in_=o0[:], func=ACT.Copy, scale=Y_SCALE, saturate=False)
+            nc.sync.dma_start(out=out_0.rearrange("(t p) c -> p t c", p=P)[:, :, IN_F:IN_F + J], in_=o0[:])
+            for t in range(2):
+                nc.sync.dma_start(out=out_1[t * P:(t + 1) * P, IN_F:IN_F + J], in_=o8[:, t, :].bitcast(U8))

@@ -18,11 +18,13 @@ ACT = mybir.ActivationFunctionType
 
 P = 128
 PASSES = 4
-NV = 120
+NP1 = 32
+NP2 = 104
+NP3 = 120
 RV = 8
-RG = 4
+RB = 4
 KV = 10
-LG = N - 1 - NV
+NX = N + P
 
 
 def tile_minibatchdiscriminator_kernel(tc, tensor, T, out_0, out_1):
@@ -33,12 +35,12 @@ def tile_minibatchdiscriminator_kernel(tc, tensor, T, out_0, out_1):
 
         ident = cst.tile([P, P], F32, name="ident")
         rowsum = cst.tile([P, N], F32, name="rowsum")
-        colsum = cst.tile([P, N], F32, name="colsum")
-        sneg = cst.tile([P, N], F32, name="sneg")
+        colx = cst.tile([P, NX], F32, name="colx")
+        snegx = cst.tile([P, NX], F32, name="snegx")
         ssum = cst.tile([P, N], F32, name="ssum")
-        fs = cst.tile([P, K, N], F32, name="fs")
-        ev = [cst.tile([P, RV, N], F32, name="ev%d" % i) for i in range(3)]
-        eg = [cst.tile([P, RG, LG], F32, name="eg%d" % i) for i in range(2)]
+        fsx = cst.tile([P, K, NX], F32, name="fsx")
+        zero = cst.tile([P, NX], F32, name="zero")
+        onesz = cst.tile([P, 1], F32, name="onesz")
         xs = [cst.tile([P, IN_F], BF16, name="xs%d" % t) for t in range(2)]
 
         for t in range(2):
@@ -46,11 +48,9 @@ def tile_minibatchdiscriminator_kernel(tc, tensor, T, out_0, out_1):
 
         make_identity(nc, ident[:])
         nc.gpsimd.memset(rowsum[:], 0.0)
-        nc.gpsimd.memset(colsum[:], 0.0)
-        for e in ev:
-            nc.gpsimd.memset(e[:, :, 0:RV], 0.0)
-        for e in eg:
-            nc.gpsimd.memset(e[:, :, 0:RG], 0.0)
+        nc.gpsimd.memset(colx[:], 0.0)
+        nc.gpsimd.memset(zero[:], 0.0)
+        nc.vector.tensor_scalar(out=onesz[:], in0=ident[:, P - 1:P], scalar1=-1.0, scalar2=1.0, op0=ALU.mult, op1=ALU.add)
 
         fp = []
         with ExitStack() as pre:
@@ -117,86 +117,83 @@ def tile_minibatchdiscriminator_kernel(tc, tensor, T, out_0, out_1):
                     mm(2 * b + 1, s)
 
         for b in range(8):
-            nc.scalar.copy(out=fs[:, 2 * b:2 * b + 2, :], in_=fp[b][:])
-            for kk in range(2):
-                for hf in range(2):
-                    cs = slice(hf * P, (hf + 1) * P)
-                    if b == 0 and kk == 0:
-                        nc.vector.tensor_scalar(out=sneg[:, cs], in0=fp[b][:, kk, cs], scalar1=-0.5, scalar2=None, op0=ALU.mult)
-                    else:
-                        nc.vector.scalar_tensor_tensor(out=sneg[:, cs], in0=fp[b][:, kk, cs], scalar=-0.5, in1=sneg[:, cs], op0=ALU.mult, op1=ALU.add)
-        nc.scalar.activation(out=ssum[:], in_=sneg[:], func=ACT.Copy, scale=-2.0)
+            if b % 2 == 0:
+                nc.scalar.copy(out=fsx[:, 2 * b:2 * b + 2, 0:N], in_=fp[b][:])
+                nc.scalar.copy(out=fsx[:, 2 * b:2 * b + 2, N:NX], in_=fp[b][:, :, 0:P])
+            else:
+                nc.vector.tensor_copy(out=fsx[:, 2 * b:2 * b + 2, 0:N], in_=fp[b][:])
+                nc.vector.tensor_copy(out=fsx[:, 2 * b:2 * b + 2, N:NX], in_=fp[b][:, :, 0:P])
+        nc.vector.tensor_reduce(out=ssum[:], in_=fsx[:, :, 0:N].rearrange("p k m -> p m k"), axis=mybir.AxisListType.X, op=ALU.add)
+        nc.vector.tensor_scalar(out=snegx[:, 0:N], in0=ssum[:], scalar1=-0.5, scalar2=None, op0=ALU.mult)
+        nc.vector.tensor_scalar(out=snegx[:, N:NX], in0=ssum[:, 0:P], scalar1=-0.5, scalar2=None, op0=ALU.mult)
 
         with ExitStack() as mainctx:
-            apool = mainctx.enter_context(tc.tile_pool(name="apool", bufs=3))
-            accp = mainctx.enter_context(tc.tile_pool(name="accp", bufs=3))
+            tpool = mainctx.enter_context(tc.tile_pool(name="tpool", bufs=14))
+            epool = mainctx.enter_context(tc.tile_pool(name="epool", bufs=3))
+            accp = mainctx.enter_context(tc.tile_pool(name="accp", bufs=2))
             xop = mainctx.enter_context(tc.tile_pool(name="xop", bufs=2))
 
-            vgroups = list(range(0, NV, RV))
-            ggroups = list(range(NV, N, RG))
-            accs = {}
-            atiles = {}
+            s1 = psum.tile([P, NX], F32, name="s1", tag="b4")
+            s2 = psum.tile([P, N], F32, name="s2", tag="b5")
+            nc.tensor.matmul(out=s1[:], lhsT=zero[:, 0:P], rhs=zero[:], start=True, stop=False)
+            nc.tensor.matmul(out=s2[:], lhsT=zero[:, 0:P], rhs=zero[:, 0:N], start=True, stop=False)
 
-            def vs(i):
-                n0 = vgroups[i]
-                lg = N - 1 - n0
-                acc = accp.tile([P, RV, N], F32, name="acc", tag="acc")
-                accs[i] = acc
+            def p1_sum(n0):
+                acc = accp.tile([P, RV, P], F32, name="acc", tag="acc")
                 for k in range(K):
                     for r in range(RV):
                         n = n0 + r
                         nc.vector.scalar_tensor_tensor(
-                            out=acc[:, r, r:lg],
-                            in0=fp[k // 2][:, k % 2, n + 1:N],
-                            scalar=fs[:, k, n:n + 1],
-                            in1=(sneg[:, n + 1:N] if k == 0 else acc[:, r, r:lg]),
+                            out=acc[:, r, :],
+                            in0=fsx[:, k, n + 1:n + 1 + P],
+                            scalar=fsx[:, k, n:n + 1],
+                            in1=(snegx[:, n + 1:n + 1 + P] if k == 0 else acc[:, r, :]),
                             op0=ALU.max,
                             op1=ALU.add,
                         )
+                return acc
 
-            def ve(i):
-                n0 = vgroups[i]
-                lg = N - 1 - n0
+            def p1_finish(n0, acc):
+                e = accp.tile([P, RV, P], F32, name="e", tag="e")
                 for r in range(RV):
                     n = n0 + r
-                    nc.scalar.activation(out=ev[i % 3][:, r, r:lg], in_=accs[i][:, r, r:lg], func=ACT.Exp, scale=-2.0,
+                    nc.scalar.activation(out=e[:, r, :], in_=acc[:, r, :], func=ACT.Exp, scale=-2.0,
                                          bias=ssum[:, n:n + 1], accum_out=rowsum[:, n:n + 1])
+                nc.vector.tensor_tensor(out=rowsum[:, n0:n0 + RV], in0=rowsum[:, n0:n0 + RV], in1=e[:, :, P - 1], op=ALU.subtract)
+                for r in range(RV):
+                    n = n0 + r
+                    nc.vector.tensor_tensor(out=colx[:, n + 1:n + 1 + P], in0=colx[:, n + 1:n + 1 + P], in1=e[:, r, :], op=ALU.add)
 
-            def fold(e, rows, n0):
-                lg = N - 1 - n0
-                h = rows // 2
-                while h >= 1:
-                    nc.gpsimd.tensor_tensor(out=e[:, 0:h, 0:lg], in0=e[:, 0:h, 0:lg], in1=e[:, h:2 * h, 0:lg], op=ALU.add)
-                    h = h // 2
-                nc.gpsimd.tensor_tensor(out=colsum[:, n0 + 1:N], in0=colsum[:, n0 + 1:N], in1=e[:, 0, 0:lg], op=ALU.add)
-
-            def ga(g):
-                n0 = ggroups[g]
-                lg = N - 1 - n0
-                a = apool.tile([P, K, RG, LG], F32, name="a", tag="a")
-                atiles[g] = a
-                for r in range(RG):
+            def bank_sum(n0, kind, index):
+                lt = psum.tile([P, RB, P], F32, name="lt", tag="b%d" % (index % 4))
+                for q in range(RB):
+                    n = n0 + q
+                    a = tpool.tile([P, K, P], F32, name="a", tag="a")
+                    if kind == 2:
+                        nc.vector.tensor_tensor(out=a[:], in0=fsx[:, :, n + 1:n + 1 + P],
+                                                in1=fsx[:, :, n:n + 1].to_broadcast([P, K, P]), op=ALU.max)
+                    else:
+                        for k in range(K):
+                            nc.scalar.activation(out=a[:, k, :], in_=fsx[:, k, n + 1:n + 1 + P], func=ACT.Abs, scale=-1.0,
+                                                 bias=fsx[:, k, n:n + 1])
                     for k in range(K):
-                        nc.scalar.activation(out=a[:, k, r, 0:lg], in_=fs[:, k, n0 + 1:N], func=ACT.Abs, scale=-1.0,
-                                             bias=fs[:, k, n0 + r:n0 + r + 1])
+                        nc.tensor.matmul(out=lt[:, q, :], lhsT=a[:, k, :], rhs=ident[:], is_transpose=True,
+                                         start=(k == 0), stop=(kind == 3 and k == K - 1))
+                    if kind == 2:
+                        nc.tensor.matmul(out=lt[:, q, :], lhsT=snegx[:, n + 1:n + 1 + P], rhs=ident[:], is_transpose=True,
+                                         start=False, stop=False)
+                        nc.tensor.matmul(out=lt[:, q, :], lhsT=snegx[:, n:n + 1].to_broadcast([P, P]), rhs=ident[:], is_transpose=True,
+                                         start=False, stop=True)
+                return lt
 
-            def gt(g):
-                n0 = ggroups[g]
-                lg = N - 1 - n0
-                a = atiles[g]
-                h = K // 2
-                while h >= 1:
-                    nc.gpsimd.tensor_tensor(out=a[:, 0:h, :, 0:lg], in0=a[:, 0:h, :, 0:lg], in1=a[:, h:2 * h, :, 0:lg], op=ALU.add)
-                    h = h // 2
-
-            def ge(g):
-                n0 = ggroups[g]
-                lg = N - 1 - n0
-                for r in range(RG):
-                    if r < lg:
-                        n = n0 + r
-                        nc.scalar.activation(out=eg[g % 2][:, r, r:lg], in_=atiles[g][:, 0, r, r:lg], func=ACT.Exp, scale=-1.0,
-                                             accum_out=rowsum[:, n:n + 1])
+            def bank_finish(n0, kind, lt):
+                et = epool.tile([P, RB, P], F32, name="et", tag="et")
+                nc.scalar.activation(out=et[:], in_=lt[:], func=ACT.Exp, scale=(-2.0 if kind == 2 else -1.0))
+                for q in range(RB):
+                    n = n0 + q
+                    nc.tensor.matmul(out=s2[:, n:n + 1], lhsT=et[:, q, :], rhs=onesz[:], start=False, stop=False)
+                    nc.tensor.matmul(out=s1[:, n + 1:n + 1 + P], lhsT=et[:, q, :], rhs=ident[:], is_transpose=True,
+                                     start=False, stop=False)
 
             def xout(t):
                 xf = xop.tile([P, IN_F], F32, name="xf", tag="xf")
@@ -206,61 +203,58 @@ def tile_minibatchdiscriminator_kernel(tc, tensor, T, out_0, out_1):
                 nc.scalar.activation(out=x8[:], in_=xf[:], func=ACT.Copy, scale=Y_SCALE, saturate=False)
                 nc.sync.dma_start(out=out_1[t * P:(t + 1) * P, 0:IN_F], in_=x8[:].bitcast(U8))
 
-            def cost_v(i):
-                return sum(K * (N - 1 - vgroups[i] - r + 18) for r in range(RV))
+            want = {1: NP1 // RV, 2: NP2 // RB, 3: NP3 // RB}
+            total = want[1] + want[2] + want[3]
+            given = {1: 0, 2: 0, 3: 0}
+            order = []
+            for step in range(total):
+                kind = max((3, 2, 1), key=lambda c: want[c] * (step + 1) - given[c] * total)
+                given[kind] += 1
+                order.append(kind)
 
-            def cost_g(g):
-                return 2 * (K + 1) * RG * (N - 1 - ggroups[g]) + 1200
-
-            ng = len(ggroups)
-            nvg = len(vgroups)
-            ga(0)
-            ga(1)
-            clock_g = 0
-            clock_v = 0
-            iv = 0
-            done_at = []
-            next_ve = 0
-            for g in range(ng):
-                if g >= 1:
-                    ge(g - 1)
-                first_ve = next_ve
-                while next_ve < iv and done_at[next_ve] <= clock_g:
-                    ve(next_ve)
-                    next_ve += 1
-                while iv < nvg and clock_v <= clock_g + cost_g(g) and iv - next_ve < 3:
-                    vs(iv)
-                    clock_v += cost_v(iv)
-                    done_at.append(clock_v)
-                    iv += 1
-                if g + 2 < ng:
-                    ga(g + 2)
-                if g in (2, 4):
-                    xout(g // 2 - 1)
-                gt(g)
-                clock_g += cost_g(g)
-                if g >= 1:
-                    fold(eg[(g - 1) % 2], RG, ggroups[g - 1])
-                for i in range(first_ve, next_ve):
-                    fold(ev[i % 3], RV, vgroups[i])
-                    clock_g += 2 * RV * (N - 1 - vgroups[i])
-            ge(ng - 1)
-            fold(eg[(ng - 1) % 2], RG, ggroups[ng - 1])
-            while next_ve < nvg:
-                if iv < nvg and iv - next_ve < 2:
-                    vs(iv)
-                    iv += 1
+            row = 0
+            banks = []
+            banks_done = 0
+            groups = []
+            groups_done = 0
+            for step in range(total):
+                kind = order[step]
+                if kind == 1:
+                    groups.append((row, p1_sum(row)))
+                    row += RV
+                    if len(groups) - groups_done > 1:
+                        p1_finish(*groups[groups_done])
+                        groups_done += 1
                 else:
-                    ve(next_ve)
-                    fold(ev[next_ve % 3], RV, vgroups[next_ve])
-                    next_ve += 1
+                    banks.append((row, kind, bank_sum(row, kind, len(banks))))
+                    row += RB
+                    if len(banks) - banks_done > 2:
+                        bank_finish(*banks[banks_done])
+                        banks_done += 1
+                if step in (6, 12):
+                    xout(step // 6 - 1)
+            for item in banks[banks_done:]:
+                bank_finish(*item)
+            for item in groups[groups_done:]:
+                p1_finish(*item)
+            assert row == N
+
+            nc.tensor.matmul(out=s1[:], lhsT=zero[:, 0:P], rhs=zero[:], start=False, stop=True)
+            nc.tensor.matmul(out=s2[:], lhsT=zero[:, 0:P], rhs=zero[:, 0:N], start=False, stop=True)
+            s1c = xop.tile([P, NX], F32, name="s1c", tag="s1c")
+            s2c = xop.tile([P, N], F32, name="s2c", tag="s2c")
+            nc.vector.tensor_copy(out=s1c[:], in_=s1[:])
+            nc.scalar.copy(out=s2c[:], in_=s2[:])
 
             o0 = xop.tile([P, 2, J], F32, name="o0", tag="o0")
             o8 = xop.tile([P, 2, J], FP8, name="o8", tag="o8")
-            pt = psum.tile([P, 2, J], F32, name="pt", tag="b0")
+            pt = psum.tile([P, 2, J], F32, name="pt", tag="b6")
             for t in range(2):
-                nc.tensor.matmul(out=pt[:, t, :], lhsT=rowsum[:, t * P:(t + 1) * P], rhs=ident[:], is_transpose=True, start=True, stop=False)
-                nc.tensor.matmul(out=pt[:, t, :], lhsT=colsum[:, t * P:(t + 1) * P], rhs=ident[:], is_transpose=True, start=False, stop=True)
+                parts = [rowsum[:, t * P:(t + 1) * P], colx[:, t * P:(t + 1) * P], s2c[:, t * P:(t + 1) * P], s1c[:, t * P:(t + 1) * P]]
+                if t == 0:
+                    parts = parts + [colx[:, N:NX], s1c[:, N:NX]]
+                for i in range(len(parts)):
+                    nc.tensor.matmul(out=pt[:, t, :], lhsT=parts[i], rhs=ident[:], is_transpose=True, start=(i == 0), stop=(i == len(parts) - 1))
             nc.vector.tensor_scalar(out=o0[:], in0=pt[:], scalar1=1.0, scalar2=None, op0=ALU.add)
             nc.scalar.activation(out=o8[:], in_=o0[:], func=ACT.Copy, scale=Y_SCALE, saturate=False)
             nc.sync.dma_start(out=out_0.rearrange("(t p) c -> p t c", p=P)[:, :, IN_F:IN_F + J], in_=o0[:])

@@ -18,9 +18,9 @@ ACT = mybir.ActivationFunctionType
 
 P = 128
 PASSES = 4
-NP1 = 32
-NP2 = 104
-NP3 = 120
+NP1 = 120
+NP2 = 0
+NP3 = 136
 RV = 8
 RB = 4
 KV = 10

@@ -23,7 +23,7 @@ NP2 = 0
 NP3 = 136
 RV = 8
 RB = 4
-KV = 10
+CV = 640
 NX = N + P
 
 
@@ -38,6 +38,7 @@ def tile_minibatchdiscriminator_kernel(tc, tensor, T, out_0, out_1):
         colx = cst.tile([P, NX], F32, name="colx")
         snegx = cst.tile([P, NX], F32, name="snegx")
         ssum = cst.tile([P, N], F32, name="ssum")
+        half = cst.tile([P, 2, N], F32, name="half")
         fsx = cst.tile([P, K, NX], F32, name="fsx")
         zero = cst.tile([P, NX], F32, name="zero")
         onesz = cst.tile([P, 1], F32, name="onesz")
@@ -55,13 +56,14 @@ def tile_minibatchdiscriminator_kernel(tc, tensor, T, out_0, out_1):
         fp = []
         with ExitStack() as pre:
             rawp = pre.enter_context(tc.tile_pool(name="rawp", bufs=4))
-            grpp = pre.enter_context(tc.tile_pool(name="grpp", bufs=2))
+            grpp = pre.enter_context(tc.tile_pool(name="grpp", bufs=3))
             keep = pre.enter_context(tc.tile_pool(name="keep", bufs=1))
             tq = keep.tile([P, PASSES, J * K], U32, name="tq", align_bytes=64)
             tsc = keep.tile([P, PASSES, J * K], U8, name="tsc", align_bytes=64)
             xg = keep.tile([P, PASSES, N, 4], BF16, name="xg", align_bytes=64)
             xq = keep.tile([P, PASSES * N], U32, name="xq", align_bytes=64)
             xsc = keep.tile([P, PASSES * N], U8, name="xsc", align_bytes=64)
+            fnat = [keep.tile([P, K, J], F32, name="fnat%d" % t) for t in range(2)]
 
             tv = T.rearrange("(s p t) j k -> s p t (j k)", p=P, t=4)
             raws = []
@@ -80,52 +82,54 @@ def tile_minibatchdiscriminator_kernel(tc, tensor, T, out_0, out_1):
                 nc.vector.tensor_copy(out=xg[:, g, :, :].bitcast(F32), in_=xt[:].rearrange("p u n -> p n u"))
             nc.vector.quantize_mx(out=xq[:].bitcast(FP8X4), scales=xsc[:], in_=xg[:].rearrange("p g n f -> p (g n f)"))
 
+            ft = [psum.tile([P, 512], F32, name="ft", tag="b%d" % b) for b in range(8)]
+            for s in range(PASSES):
+                for h in range(2):
+                    grp = grpp.tile([P, 1024, 4], BF16, name="grp", tag="grp", align_bytes=64)
+                    src = raws[2 * s + h][:].rearrange("p t c -> p c t")
+                    nc.vector.tensor_copy(out=grp[:, 0:CV, :], in_=src[:, 0:CV, :])
+                    nc.scalar.copy(out=grp[:, CV:1024, :], in_=src[:, CV:1024, :])
+                    cols = slice(1024 * h, 1024 * (h + 1))
+                    nc.vector.quantize_mx(out=tq[:, s, cols].bitcast(FP8X4), scales=tsc[:, s, cols],
+                                          in_=grp[:].rearrange("p c t -> p (c t)"))
+                    for w in range(2 * h, 2 * h + 2):
+                        for t in range(2):
+                            nc.tensor.matmul_mx(
+                                out=ft[4 * t + w][:],
+                                lhsT=xq[:, s * N + t * P:s * N + (t + 1) * P].bitcast(FP8X4),
+                                lhsT_scale=xsc[:, s * N + t * P:s * N + (t + 1) * P],
+                                rhs=tq[:, s, 512 * w:512 * (w + 1)].bitcast(FP8X4),
+                                rhs_scale=tsc[:, s, 512 * w:512 * (w + 1)],
+                                start=(s == 0),
+                                stop=(s == PASSES - 1),
+                            )
+            for w in range(4):
+                for t in range(2):
+                    dst = fnat[t][:, :, 32 * w:32 * (w + 1)]
+                    view = ft[4 * t + w][:].rearrange("p (j k) -> p k j", k=K)
+                    if t == 0:
+                        nc.vector.tensor_copy(out=dst, in_=view)
+                    else:
+                        nc.scalar.copy(out=dst, in_=view)
             for b in range(8):
                 fpb = psum.tile([P, 2, N], F32, name="fp", tag="b%d" % b)
                 fp.append(fpb)
+                for kk in range(2):
+                    for t in range(2):
+                        nc.tensor.transpose(fpb[:, kk, t * P:(t + 1) * P], fnat[t][:, 2 * b + kk, :], ident[:])
+                nc.scalar.copy(out=fsx[:, 2 * b:2 * b + 2, 0:N], in_=fpb[:])
+                for kk in range(2):
+                    if b == 0:
+                        nc.vector.tensor_scalar(out=half[:, kk, :], in0=fpb[:, kk, :], scalar1=-0.5, scalar2=None, op0=ALU.mult)
+                    else:
+                        nc.vector.scalar_tensor_tensor(out=half[:, kk, :], in0=fpb[:, kk, :], scalar=-0.5, in1=half[:, kk, :],
+                                                       op0=ALU.mult, op1=ALU.add)
+        nc.vector.tensor_tensor(out=snegx[:, 0:N], in0=half[:, 0, :], in1=half[:, 1, :], op=ALU.add)
+        nc.scalar.activation(out=ssum[:], in_=snegx[:, 0:N], func=ACT.Copy, scale=-2.0)
 
-            def mm(k, s):
-                nc.tensor.matmul_mx(
-                    out=fp[k // 2][:, k % 2, :],
-                    lhsT=tq[:, s, k * J:(k + 1) * J].bitcast(FP8X4),
-                    lhsT_scale=tsc[:, s, k * J:(k + 1) * J],
-                    rhs=xq[:, s * N:(s + 1) * N].bitcast(FP8X4),
-                    rhs_scale=xsc[:, s * N:(s + 1) * N],
-                    start=(s == 0),
-                    stop=(s == PASSES - 1),
-                )
-
-            for s in range(PASSES):
-                grp = grpp.tile([P, K, J, 4], BF16, name="grp", tag="grp", align_bytes=64)
-                for h in range(2):
-                    src = raws[2 * s + h][:].rearrange("p t (j k) -> p k j t", k=K)
-                    js = slice(64 * h, 64 * h + 64)
-                    nc.vector.tensor_copy(out=grp[:, 0:KV, js, :], in_=src[:, 0:KV, :, :])
-                    nc.scalar.copy(out=grp[:, KV:K, js, :], in_=src[:, KV:K, :, :])
-                for q in range(2):
-                    nc.vector.quantize_mx(
-                        out=tq[:, s, 1024 * q:1024 * (q + 1)].bitcast(FP8X4),
-                        scales=tsc[:, s, 1024 * q:1024 * (q + 1)],
-                        in_=grp[:, 8 * q:8 * (q + 1), :, :].rearrange("p k j t -> p (k j t)"),
-                    )
-                if s < PASSES - 1:
-                    for b in range(8):
-                        mm(2 * b, s)
-            for b in range(8):
-                mm(2 * b, PASSES - 1)
-                for s in range(PASSES):
-                    mm(2 * b + 1, s)
-
-        for b in range(8):
-            if b % 2 == 0:
-                nc.scalar.copy(out=fsx[:, 2 * b:2 * b + 2, 0:N], in_=fp[b][:])
-                nc.scalar.copy(out=fsx[:, 2 * b:2 * b + 2, N:NX], in_=fp[b][:, :, 0:P])
-            else:
-                nc.vector.tensor_copy(out=fsx[:, 2 * b:2 * b + 2, 0:N], in_=fp[b][:])
-                nc.vector.tensor_copy(out=fsx[:, 2 * b:2 * b + 2, N:NX], in_=fp[b][:, :, 0:P])
-        nc.vector.tensor_reduce(out=ssum[:], in_=fsx[:, :, 0:N].rearrange("p k m -> p m k"), axis=mybir.AxisListType.X, op=ALU.add)
-        nc.vector.tensor_scalar(out=snegx[:, 0:N], in0=ssum[:], scalar1=-0.5, scalar2=None, op0=ALU.mult)
-        nc.vector.tensor_scalar(out=snegx[:, N:NX], in0=ssum[:, 0:P], scalar1=-0.5, scalar2=None, op0=ALU.mult)
+        def wrap():
+            nc.scalar.copy(out=fsx[:, :, N:NX], in_=fsx[:, :, 0:P])
+            nc.scalar.copy(out=snegx[:, N:NX], in_=snegx[:, 0:P])
 
         with ExitStack() as mainctx:
             tpool = mainctx.enter_context(tc.tile_pool(name="tpool", bufs=14))
@@ -231,6 +235,8 @@ def tile_minibatchdiscriminator_kernel(tc, tensor, T, out_0, out_1):
                     if len(banks) - banks_done > 2:
                         bank_finish(*banks[banks_done])
                         banks_done += 1
+                if step == 2:
+                    wrap()
                 if step in (6, 12):
                     xout(step // 6 - 1)
             for item in banks[banks_done:]:

@@ -18,9 +18,8 @@ ACT = mybir.ActivationFunctionType
 
 P = 128
 PASSES = 4
-NP1 = 120
-NP2 = 0
-NP3 = 136
+NP1 = 136
+NP3 = 120
 RV = 8
 RB = 4
 CV = 640
@@ -134,7 +133,7 @@ def tile_minibatchdiscriminator_kernel(tc, tensor, T, out_0, out_1):
         with ExitStack() as mainctx:
             tpool = mainctx.enter_context(tc.tile_pool(name="tpool", bufs=14))
             epool = mainctx.enter_context(tc.tile_pool(name="epool", bufs=3))
-            accp = mainctx.enter_context(tc.tile_pool(name="accp", bufs=2))
+            accp = mainctx.enter_context(tc.tile_pool(name="accp", bufs=3))
             xop = mainctx.enter_context(tc.tile_pool(name="xop", bufs=2))
 
             s1 = psum.tile([P, NX], F32, name="s1", tag="b4")
@@ -142,7 +141,14 @@ def tile_minibatchdiscriminator_kernel(tc, tensor, T, out_0, out_1):
             nc.tensor.matmul(out=s1[:], lhsT=zero[:, 0:P], rhs=zero[:], start=True, stop=False)
             nc.tensor.matmul(out=s2[:], lhsT=zero[:, 0:P], rhs=zero[:, 0:N], start=True, stop=False)
 
-            def p1_sum(n0):
+            def p1_add(n0, e, i):
+                if i == 0:
+                    nc.vector.tensor_tensor(out=rowsum[:, n0:n0 + RV], in0=rowsum[:, n0:n0 + RV], in1=e[:, :, P - 1], op=ALU.subtract)
+                else:
+                    n = n0 + i - 1
+                    nc.vector.tensor_tensor(out=colx[:, n + 1:n + 1 + P], in0=colx[:, n + 1:n + 1 + P], in1=e[:, i - 1, :], op=ALU.add)
+
+            def p1_sum(n0, late):
                 acc = accp.tile([P, RV, P], F32, name="acc", tag="acc")
                 for k in range(K):
                     for r in range(RV):
@@ -155,49 +161,40 @@ def tile_minibatchdiscriminator_kernel(tc, tensor, T, out_0, out_1):
                             op0=ALU.max,
                             op1=ALU.add,
                         )
+                    if late is not None and k <= RV:
+                        p1_add(late[0], late[1], k)
                 return acc
 
-            def p1_finish(n0, acc):
+            def p1_exp(n0, acc):
                 e = accp.tile([P, RV, P], F32, name="e", tag="e")
                 for r in range(RV):
                     n = n0 + r
                     nc.scalar.activation(out=e[:, r, :], in_=acc[:, r, :], func=ACT.Exp, scale=-2.0,
                                          bias=ssum[:, n:n + 1], accum_out=rowsum[:, n:n + 1])
-                nc.vector.tensor_tensor(out=rowsum[:, n0:n0 + RV], in0=rowsum[:, n0:n0 + RV], in1=e[:, :, P - 1], op=ALU.subtract)
-                for r in range(RV):
-                    n = n0 + r
-                    nc.vector.tensor_tensor(out=colx[:, n + 1:n + 1 + P], in0=colx[:, n + 1:n + 1 + P], in1=e[:, r, :], op=ALU.add)
+                return e
 
-            def bank_sum(n0, kind, index):
+            def bank_sum(n0, index):
                 lt = psum.tile([P, RB, P], F32, name="lt", tag="b%d" % (index % 4))
                 for q in range(RB):
                     n = n0 + q
                     a = tpool.tile([P, K, P], F32, name="a", tag="a")
-                    if kind == 2:
-                        nc.vector.tensor_tensor(out=a[:], in0=fsx[:, :, n + 1:n + 1 + P],
-                                                in1=fsx[:, :, n:n + 1].to_broadcast([P, K, P]), op=ALU.max)
-                    else:
-                        for k in range(K):
-                            nc.scalar.activation(out=a[:, k, :], in_=fsx[:, k, n + 1:n + 1 + P], func=ACT.Abs, scale=-1.0,
-                                                 bias=fsx[:, k, n:n + 1])
+                    for k in range(K):
+                        nc.scalar.activation(out=a[:, k, :], in_=fsx[:, k, n + 1:n + 1 + P], func=ACT.Abs, scale=-1.0,
+                                             bias=fsx[:, k, n:n + 1])
                     for k in range(K):
                         nc.tensor.matmul(out=lt[:, q, :], lhsT=a[:, k, :], rhs=ident[:], is_transpose=True,
-                                         start=(k == 0), stop=(kind == 3 and k == K - 1))
-                    if kind == 2:
-                        nc.tensor.matmul(out=lt[:, q, :], lhsT=snegx[:, n + 1:n + 1 + P], rhs=ident[:], is_transpose=True,
-                                         start=False, stop=False)
-                        nc.tensor.matmul(out=lt[:, q, :], lhsT=snegx[:, n:n + 1].to_broadcast([P, P]), rhs=ident[:], is_transpose=True,
-                                         start=False, stop=True)
+                                         start=(k == 0), stop=(k == K - 1))
                 return lt
 
-            def bank_finish(n0, kind, lt):
+            def bank_finish(n0, lt, last):
                 et = epool.tile([P, RB, P], F32, name="et", tag="et")
-                nc.scalar.activation(out=et[:], in_=lt[:], func=ACT.Exp, scale=(-2.0 if kind == 2 else -1.0))
+                nc.scalar.activation(out=et[:], in_=lt[:], func=ACT.Exp, scale=-1.0)
                 for q in range(RB):
                     n = n0 + q
-                    nc.tensor.matmul(out=s2[:, n:n + 1], lhsT=et[:, q, :], rhs=onesz[:], start=False, stop=False)
+                    end = last and q == RB - 1
+                    nc.tensor.matmul(out=s2[:, n:n + 1], lhsT=et[:, q, :], rhs=onesz[:], start=False, stop=end)
                     nc.tensor.matmul(out=s1[:, n + 1:n + 1 + P], lhsT=et[:, q, :], rhs=ident[:], is_transpose=True,
-                                     start=False, stop=False)
+                                     start=False, stop=end)
 
             def xout(t):
                 xf = xop.tile([P, IN_F], F32, name="xf", tag="xf")
@@ -207,46 +204,45 @@ def tile_minibatchdiscriminator_kernel(tc, tensor, T, out_0, out_1):
                 nc.scalar.activation(out=x8[:], in_=xf[:], func=ACT.Copy, scale=Y_SCALE, saturate=False)
                 nc.sync.dma_start(out=out_1[t * P:(t + 1) * P, 0:IN_F], in_=x8[:].bitcast(U8))
 
-            want = {1: NP1 // RV, 2: NP2 // RB, 3: NP3 // RB}
-            total = want[1] + want[2] + want[3]
-            given = {1: 0, 2: 0, 3: 0}
+            want = {1: NP1 // RV, 3: NP3 // RB}
+            total = want[1] + want[3]
+            given = {1: 0, 3: 0}
             order = []
             for step in range(total):
-                kind = max((3, 2, 1), key=lambda c: want[c] * (step + 1) - given[c] * total)
+                kind = max((3, 1), key=lambda c: want[c] * (step + 1) - given[c] * total)
                 given[kind] += 1
                 order.append(kind)
 
             row = 0
             banks = []
             banks_done = 0
-            groups = []
-            groups_done = 0
-            for step in range(total):
-                kind = order[step]
-                if kind == 1:
-                    groups.append((row, p1_sum(row)))
-                    row += RV
-                    if len(groups) - groups_done > 1:
-                        p1_finish(*groups[groups_done])
-                        groups_done += 1
-                else:
-                    banks.append((row, kind, bank_sum(row, kind, len(banks))))
-                    row += RB
-                    if len(banks) - banks_done > 2:
-                        bank_finish(*banks[banks_done])
-                        banks_done += 1
-                if step == 2:
-                    wrap()
-                if step in (6, 12):
-                    xout(step // 6 - 1)
-            for item in banks[banks_done:]:
-                bank_finish(*item)
-            for item in groups[groups_done:]:
-                p1_finish(*item)
+            sums = []
+            exps = []
+            with tc.manual_schedule(engines={mybir.EngineType.DVE}):
+                for step in range(total):
+                    if order[step] == 1:
+                        if len(sums) > len(exps):
+                            exps.append((sums[-1][0], p1_exp(*sums[-1])))
+                        sums.append((row, p1_sum(row, exps[-2] if len(exps) > 1 else None)))
+                        row += RV
+                    else:
+                        banks.append((row, bank_sum(row, len(banks))))
+                        row += RB
+                        if len(banks) - banks_done > 2:
+                            bank_finish(banks[banks_done][0], banks[banks_done][1], False)
+                            banks_done += 1
+                    if step == 2:
+                        wrap()
+                    if step in (6, 12):
+                        xout(step // 6 - 1)
+                exps.append((sums[-1][0], p1_exp(*sums[-1])))
+                for item in exps[-2:]:
+                    for i in range(RV + 1):
+                        p1_add(item[0], item[1], i)
+                for item in banks[banks_done:]:
+                    bank_finish(item[0], item[1], item is banks[-1])
             assert row == N
 
-            nc.tensor.matmul(out=s1[:], lhsT=zero[:, 0:P], rhs=zero[:], start=False, stop=True)
-            nc.tensor.matmul(out=s2[:], lhsT=zero[:, 0:P], rhs=zero[:, 0:N], start=False, stop=True)
             s1c = xop.tile([P, NX], F32, name="s1c", tag="s1c")
             s2c = xop.tile([P, N], F32, name="s2c", tag="s2c")
             nc.vector.tensor_copy(out=s1c[:], in_=s1[:])

@@ -18,12 +18,109 @@ ACT = mybir.ActivationFunctionType
 
 P = 128
 PASSES = 4
-NP1 = 136
-NP3 = 120
+NA = 100
+NB = 84
+NC = 72
 RV = 8
 RB = 4
 CV = 640
 NX = N + P
+TB = 12
+WARM_EVERY = 288
+WARM_FIRST = 32
+WARM_N = 4
+
+
+def build_program():
+    prog = []
+    steps = (NC // RV) * K
+    rows = []
+    banks = []
+    open_bank = {"A": None, "B": None}
+    made = []
+    state = {"row": 0, "pe": 0, "taken": 0}
+    cur = {"A": None, "B": None}
+    left = {"A": NA, "B": NB}
+    exp_due = {}
+    fin_due = {}
+    groups = []
+
+    def new_row(kind):
+        if open_bank[kind] is None or open_bank[kind][1] == RB:
+            banks.append(kind)
+            open_bank[kind] = [len(banks) - 1, 0]
+        bank, q = open_bank[kind]
+        open_bank[kind][1] += 1
+        rows.append((kind, state["row"], bank, q))
+        state["row"] += 1
+        left[kind] -= 1
+        return len(rows) - 1
+
+    def make(kind, count, step):
+        for i in range(count):
+            if cur[kind] is None:
+                if left[kind] == 0:
+                    return
+                cur[kind] = [new_row(kind), 0]
+            rid, k = cur[kind]
+            prog.append(("abs" if kind == "A" else "ts", rid, k))
+            made.append((step, rid, k))
+            cur[kind][1] += 1
+            if cur[kind][1] == K:
+                cur[kind] = None
+
+    def pe(item):
+        prog.append(item)
+        state["pe"] += 1
+        if state["pe"] % WARM_EVERY == WARM_FIRST:
+            for i in range(WARM_N):
+                prog.append(("warm",))
+
+    def share(total, step):
+        return (step + 1) * total // steps - step * total // steps
+
+    for step in range(steps + 6):
+        if step < steps:
+            g, k = divmod(step, K)
+            if k == 0:
+                groups.append(state["row"])
+                state["row"] += RV
+            for r in range(RV):
+                prog.append(("stt", g, k, r))
+            if g >= 2 and k <= RV:
+                prog.append(("cadd", g - 2, k))
+            make("B", share(NB * K, step), step)
+            if g >= 1 and 1 <= k <= RV:
+                prog.append(("cexp", g - 1, k - 1))
+            make("A", share(NA * K, step), step)
+            if step == 2:
+                prog.append(("wrap",))
+            if step in (24, 48):
+                prog.append(("xout", step // 24 - 1))
+        for bank in exp_due.get(step, []):
+            prog.append(("bexp", bank))
+            fin_due.setdefault(step + 1, []).append(bank)
+        for bank in fin_due.get(step, []):
+            for q in range(RB):
+                pe(("fin", bank, q))
+        while state["taken"] < len(made) and made[state["taken"]][0] < step:
+            st, rid, k = made[state["taken"]]
+            state["taken"] += 1
+            kind, n, bank, q = rows[rid]
+            if kind == "B" and k == 0:
+                pe(("tp", rid, -1))
+            pe(("tp", rid, k))
+            if k == K - 1 and q == RB - 1:
+                exp_due.setdefault(step + 1, []).append(bank)
+    ng = len(groups)
+    for r in range(RV):
+        prog.append(("cexp", ng - 1, r))
+    for g in (ng - 2, ng - 1):
+        for i in range(RV + 1):
+            prog.append(("cadd", g, i))
+    assert state["row"] == N and state["taken"] == len(made) == (NA + NB) * K
+    assert max(fin_due) < steps + 6
+    return prog, rows, banks, groups
 
 
 def tile_minibatchdiscriminator_kernel(tc, tensor, T, out_0, out_1):
@@ -39,9 +136,14 @@ def tile_minibatchdiscriminator_kernel(tc, tensor, T, out_0, out_1):
         ssum = cst.tile([P, N], F32, name="ssum")
         half = cst.tile([P, 2, N], F32, name="half")
         fsx = cst.tile([P, K, NX], F32, name="fsx")
-        zero = cst.tile([P, NX], F32, name="zero")
+        hneg = cst.tile([P, K, N], F32, name="hneg")
+        zero = cst.tile([P, NX + 2], F32, name="zero")
         onesz = cst.tile([P, 1], F32, name="onesz")
         xs = [cst.tile([P, IN_F], BF16, name="xs%d" % t) for t in range(2)]
+        xq = cst.tile([P, PASSES * N], U32, name="xq", align_bytes=64)
+        xsc = cst.tile([P, PASSES * N], U8, name="xsc", align_bytes=64)
+        tq0 = cst.tile([P, 1024], U32, name="tq0", align_bytes=64)
+        tsc0 = cst.tile([P, 1024], U8, name="tsc0", align_bytes=64)
 
         for t in range(2):
             nc.sync.dma_start(out=xs[t][:], in_=tensor[t * P:(t + 1) * P, :])
@@ -57,11 +159,9 @@ def tile_minibatchdiscriminator_kernel(tc, tensor, T, out_0, out_1):
             rawp = pre.enter_context(tc.tile_pool(name="rawp", bufs=4))
             grpp = pre.enter_context(tc.tile_pool(name="grpp", bufs=3))
             keep = pre.enter_context(tc.tile_pool(name="keep", bufs=1))
-            tq = keep.tile([P, PASSES, J * K], U32, name="tq", align_bytes=64)
-            tsc = keep.tile([P, PASSES, J * K], U8, name="tsc", align_bytes=64)
+            tqs = [tq0] + [keep.tile([P, 1024], U32, name="tq%d" % i, align_bytes=64) for i in range(1, 2 * PASSES)]
+            tscs = [tsc0] + [keep.tile([P, 1024], U8, name="tsc%d" % i, align_bytes=64) for i in range(1, 2 * PASSES)]
             xg = keep.tile([P, PASSES, N, 4], BF16, name="xg", align_bytes=64)
-            xq = keep.tile([P, PASSES * N], U32, name="xq", align_bytes=64)
-            xsc = keep.tile([P, PASSES * N], U8, name="xsc", align_bytes=64)
             fnat = [keep.tile([P, K, J], F32, name="fnat%d" % t) for t in range(2)]
 
             tv = T.rearrange("(s p t) j k -> s p t (j k)", p=P, t=4)
@@ -88,17 +188,17 @@ def tile_minibatchdiscriminator_kernel(tc, tensor, T, out_0, out_1):
                     src = raws[2 * s + h][:].rearrange("p t c -> p c t")
                     nc.vector.tensor_copy(out=grp[:, 0:CV, :], in_=src[:, 0:CV, :])
                     nc.scalar.copy(out=grp[:, CV:1024, :], in_=src[:, CV:1024, :])
-                    cols = slice(1024 * h, 1024 * (h + 1))
-                    nc.vector.quantize_mx(out=tq[:, s, cols].bitcast(FP8X4), scales=tsc[:, s, cols],
-                                          in_=grp[:].rearrange("p c t -> p (c t)"))
-                    for w in range(2 * h, 2 * h + 2):
+                    tq = tqs[2 * s + h]
+                    tsc = tscs[2 * s + h]
+                    nc.vector.quantize_mx(out=tq[:].bitcast(FP8X4), scales=tsc[:], in_=grp[:].rearrange("p c t -> p (c t)"))
+                    for w in range(2):
                         for t in range(2):
                             nc.tensor.matmul_mx(
-                                out=ft[4 * t + w][:],
+                                out=ft[4 * t + 2 * h + w][:],
                                 lhsT=xq[:, s * N + t * P:s * N + (t + 1) * P].bitcast(FP8X4),
                                 lhsT_scale=xsc[:, s * N + t * P:s * N + (t + 1) * P],
-                                rhs=tq[:, s, 512 * w:512 * (w + 1)].bitcast(FP8X4),
-                                rhs_scale=tsc[:, s, 512 * w:512 * (w + 1)],
+                                rhs=tq[:, 512 * w:512 * (w + 1)].bitcast(FP8X4),
+                                rhs_scale=tsc[:, 512 * w:512 * (w + 1)],
                                 start=(s == 0),
                                 stop=(s == PASSES - 1),
                             )
@@ -125,136 +225,139 @@ def tile_minibatchdiscriminator_kernel(tc, tensor, T, out_0, out_1):
                                                        op0=ALU.mult, op1=ALU.add)
         nc.vector.tensor_tensor(out=snegx[:, 0:N], in0=half[:, 0, :], in1=half[:, 1, :], op=ALU.add)
         nc.scalar.activation(out=ssum[:], in_=snegx[:, 0:N], func=ACT.Copy, scale=-2.0)
-
-        def wrap():
-            nc.scalar.copy(out=fsx[:, :, N:NX], in_=fsx[:, :, 0:P])
-            nc.scalar.copy(out=snegx[:, N:NX], in_=snegx[:, 0:P])
+        nc.vector.tensor_scalar(out=hneg[:], in0=fsx[:, :, 0:N], scalar1=-0.5, scalar2=None, op0=ALU.mult)
 
         with ExitStack() as mainctx:
-            tpool = mainctx.enter_context(tc.tile_pool(name="tpool", bufs=14))
-            epool = mainctx.enter_context(tc.tile_pool(name="epool", bufs=3))
+            tpool = mainctx.enter_context(tc.tile_pool(name="tpool", bufs=TB))
+            epool = mainctx.enter_context(tc.tile_pool(name="epool", bufs=4))
             accp = mainctx.enter_context(tc.tile_pool(name="accp", bufs=3))
             xop = mainctx.enter_context(tc.tile_pool(name="xop", bufs=2))
 
-            s1 = psum.tile([P, NX], F32, name="s1", tag="b4")
-            s2 = psum.tile([P, N], F32, name="s2", tag="b5")
-            nc.tensor.matmul(out=s1[:], lhsT=zero[:, 0:P], rhs=zero[:], start=True, stop=False)
+            s1 = [psum.tile([P, NX + 2], F32, name="s1", tag="b%d" % (4 + i)) for i in range(2)]
+            s2 = psum.tile([P, N], F32, name="s2", tag="b6")
+            idle = psum.tile([P, 512], F32, name="idle", tag="b7")
+            for i in range(2):
+                nc.tensor.matmul(out=s1[i][:], lhsT=zero[:, 0:P], rhs=zero[:], start=True, stop=False)
             nc.tensor.matmul(out=s2[:], lhsT=zero[:, 0:P], rhs=zero[:, 0:N], start=True, stop=False)
 
-            def p1_add(n0, e, i):
-                if i == 0:
-                    nc.vector.tensor_tensor(out=rowsum[:, n0:n0 + RV], in0=rowsum[:, n0:n0 + RV], in1=e[:, :, P - 1], op=ALU.subtract)
-                else:
-                    n = n0 + i - 1
-                    nc.vector.tensor_tensor(out=colx[:, n + 1:n + 1 + P], in0=colx[:, n + 1:n + 1 + P], in1=e[:, i - 1, :], op=ALU.add)
+            prog, rows, banks, groups = build_program()
+            last_fin = {}
+            for index in range(len(prog)):
+                if prog[index][0] == "fin":
+                    rid = [r for r in range(len(rows)) if rows[r][2] == prog[index][1] and rows[r][3] == prog[index][2]][0]
+                    last_fin[(rows[rid][1] + 1) % 2] = index
+                    last_fin[2] = index
+            bank_count = {"A": 0, "B": 0}
+            bank_tag = []
+            for kind in banks:
+                bank_tag.append("b%d" % ((0 if kind == "A" else 2) + bank_count[kind] % 2))
+                bank_count[kind] += 1
+            row_of = {}
+            for rid in range(len(rows)):
+                row_of[(rows[rid][2], rows[rid][3])] = rid
 
-            def p1_sum(n0, late):
-                acc = accp.tile([P, RV, P], F32, name="acc", tag="acc")
-                for k in range(K):
-                    for r in range(RV):
-                        n = n0 + r
+            terms = {}
+            lts = {}
+            ets = {}
+            accs = {}
+            es = {}
+            with tc.manual_schedule(engines={mybir.EngineType.DVE, mybir.EngineType.PE, mybir.EngineType.Activation}):
+                for index in range(len(prog)):
+                    item = prog[index]
+                    what = item[0]
+                    if what == "abs" or what == "ts":
+                        rid, k = item[1], item[2]
+                        n = rows[rid][1]
+                        if k == 0:
+                            a = tpool.tile([P, K, P], F32, name="a", tag="a")
+                            terms[rid] = a
+                        if what == "abs":
+                            nc.scalar.activation(out=terms[rid][:, k, :], in_=fsx[:, k, n + 1:n + 1 + P], func=ACT.Abs, scale=-1.0,
+                                                 bias=fsx[:, k, n:n + 1])
+                        else:
+                            nc.vector.tensor_scalar(out=terms[rid][:, k, :], in0=fsx[:, k, n + 1:n + 1 + P], scalar1=fsx[:, k, n:n + 1],
+                                                    scalar2=hneg[:, k, n:n + 1], op0=ALU.max, op1=ALU.add)
+                    elif what == "tp":
+                        rid, k = item[1], item[2]
+                        kind, n, bank, q = rows[rid]
+                        first = (k == -1) if kind == "B" else (k == 0)
+                        if first and q == 0:
+                            lt = psum.tile([P, RB, P], F32, name="lt", tag=bank_tag[bank])
+                            lts[bank] = lt
+                        nc.tensor.matmul(out=lts[bank][:, q, :], lhsT=(snegx[:, n + 1:n + 1 + P] if k == -1 else terms[rid][:, k, :]),
+                                         rhs=ident[:], is_transpose=True, start=first, stop=(k == K - 1))
+                    elif what == "bexp":
+                        bank = item[1]
+                        et = epool.tile([P, RB, P], F32, name="et", tag="et")
+                        ets[bank] = et
+                        nc.scalar.activation(out=et[:], in_=lts[bank][:], func=ACT.Exp, scale=(-1.0 if banks[bank] == "A" else -2.0))
+                    elif what == "fin":
+                        bank, q = item[1], item[2]
+                        n = rows[row_of[(bank, q)]][1]
+                        par = (n + 1) % 2
+                        nc.tensor.matmul(out=s2[:, n:n + 1], lhsT=ets[bank][:, q, :], rhs=onesz[:], start=False, stop=(last_fin[2] == index))
+                        nc.tensor.matmul(out=s1[par][:, n + 1 + par:n + 1 + par + P], lhsT=ets[bank][:, q, :], rhs=ident[:], is_transpose=True,
+                                         start=False, stop=(last_fin[par] == index))
+                    elif what == "warm":
+                        nc.tensor.matmul_mx(out=idle[:], lhsT=xq[:, 0:P].bitcast(FP8X4), lhsT_scale=xsc[:, 0:P],
+                                            rhs=tq0[:, 0:512].bitcast(FP8X4), rhs_scale=tsc0[:, 0:512], start=True, stop=True)
+                    elif what == "stt":
+                        g, k, r = item[1], item[2], item[3]
+                        n = groups[g] + r
+                        if k == 0 and r == 0:
+                            acc = accp.tile([P, RV, P], F32, name="acc", tag="acc")
+                            accs[g] = acc
                         nc.vector.scalar_tensor_tensor(
-                            out=acc[:, r, :],
+                            out=accs[g][:, r, :],
                             in0=fsx[:, k, n + 1:n + 1 + P],
                             scalar=fsx[:, k, n:n + 1],
-                            in1=(snegx[:, n + 1:n + 1 + P] if k == 0 else acc[:, r, :]),
+                            in1=(snegx[:, n + 1:n + 1 + P] if k == 0 else accs[g][:, r, :]),
                             op0=ALU.max,
                             op1=ALU.add,
                         )
-                    if late is not None and k <= RV:
-                        p1_add(late[0], late[1], k)
-                return acc
-
-            def p1_exp(n0, acc):
-                e = accp.tile([P, RV, P], F32, name="e", tag="e")
-                for r in range(RV):
-                    n = n0 + r
-                    nc.scalar.activation(out=e[:, r, :], in_=acc[:, r, :], func=ACT.Exp, scale=-2.0,
-                                         bias=ssum[:, n:n + 1], accum_out=rowsum[:, n:n + 1])
-                return e
-
-            def bank_sum(n0, index):
-                lt = psum.tile([P, RB, P], F32, name="lt", tag="b%d" % (index % 4))
-                for q in range(RB):
-                    n = n0 + q
-                    a = tpool.tile([P, K, P], F32, name="a", tag="a")
-                    for k in range(K):
-                        nc.scalar.activation(out=a[:, k, :], in_=fsx[:, k, n + 1:n + 1 + P], func=ACT.Abs, scale=-1.0,
-                                             bias=fsx[:, k, n:n + 1])
-                    for k in range(K):
-                        nc.tensor.matmul(out=lt[:, q, :], lhsT=a[:, k, :], rhs=ident[:], is_transpose=True,
-                                         start=(k == 0), stop=(k == K - 1))
-                return lt
-
-            def bank_finish(n0, lt, last):
-                et = epool.tile([P, RB, P], F32, name="et", tag="et")
-                nc.scalar.activation(out=et[:], in_=lt[:], func=ACT.Exp, scale=-1.0)
-                for q in range(RB):
-                    n = n0 + q
-                    end = last and q == RB - 1
-                    nc.tensor.matmul(out=s2[:, n:n + 1], lhsT=et[:, q, :], rhs=onesz[:], start=False, stop=end)
-                    nc.tensor.matmul(out=s1[:, n + 1:n + 1 + P], lhsT=et[:, q, :], rhs=ident[:], is_transpose=True,
-                                     start=False, stop=end)
-
-            def xout(t):
-                xf = xop.tile([P, IN_F], F32, name="xf", tag="xf")
-                x8 = xop.tile([P, IN_F], FP8, name="x8", tag="x8")
-                nc.scalar.copy(out=xf[:], in_=xs[t][:])
-                nc.sync.dma_start(out=out_0[t * P:(t + 1) * P, 0:IN_F], in_=xf[:])
-                nc.scalar.activation(out=x8[:], in_=xf[:], func=ACT.Copy, scale=Y_SCALE, saturate=False)
-                nc.sync.dma_start(out=out_1[t * P:(t + 1) * P, 0:IN_F], in_=x8[:].bitcast(U8))
-
-            want = {1: NP1 // RV, 3: NP3 // RB}
-            total = want[1] + want[3]
-            given = {1: 0, 3: 0}
-            order = []
-            for step in range(total):
-                kind = max((3, 1), key=lambda c: want[c] * (step + 1) - given[c] * total)
-                given[kind] += 1
-                order.append(kind)
-
-            row = 0
-            banks = []
-            banks_done = 0
-            sums = []
-            exps = []
-            with tc.manual_schedule(engines={mybir.EngineType.DVE}):
-                for step in range(total):
-                    if order[step] == 1:
-                        if len(sums) > len(exps):
-                            exps.append((sums[-1][0], p1_exp(*sums[-1])))
-                        sums.append((row, p1_sum(row, exps[-2] if len(exps) > 1 else None)))
-                        row += RV
+                    elif what == "cexp":
+                        g, r = item[1], item[2]
+                        n = groups[g] + r
+                        if r == 0:
+                            e = accp.tile([P, RV, P], F32, name="e", tag="e")
+                            es[g] = e
+                        nc.scalar.activation(out=es[g][:, r, :], in_=accs[g][:, r, :], func=ACT.Exp, scale=-2.0,
+                                             bias=ssum[:, n:n + 1], accum_out=rowsum[:, n:n + 1])
+                    elif what == "cadd":
+                        g, i = item[1], item[2]
+                        n0 = groups[g]
+                        if i == 0:
+                            nc.vector.tensor_tensor(out=rowsum[:, n0:n0 + RV], in0=rowsum[:, n0:n0 + RV], in1=es[g][:, :, P - 1], op=ALU.subtract)
+                        else:
+                            n = n0 + i - 1
+                            nc.vector.tensor_tensor(out=colx[:, n + 1:n + 1 + P], in0=colx[:, n + 1:n + 1 + P], in1=es[g][:, i - 1, :], op=ALU.add)
+                    elif what == "wrap":
+                        nc.scalar.copy(out=fsx[:, :, N:NX], in_=fsx[:, :, 0:P])
+                        nc.scalar.copy(out=snegx[:, N:NX], in_=snegx[:, 0:P])
                     else:
-                        banks.append((row, bank_sum(row, len(banks))))
-                        row += RB
-                        if len(banks) - banks_done > 2:
-                            bank_finish(banks[banks_done][0], banks[banks_done][1], False)
-                            banks_done += 1
-                    if step == 2:
-                        wrap()
-                    if step in (6, 12):
-                        xout(step // 6 - 1)
-                exps.append((sums[-1][0], p1_exp(*sums[-1])))
-                for item in exps[-2:]:
-                    for i in range(RV + 1):
-                        p1_add(item[0], item[1], i)
-                for item in banks[banks_done:]:
-                    bank_finish(item[0], item[1], item is banks[-1])
-            assert row == N
+                        assert what == "xout"
+                        t = item[1]
+                        xf = xop.tile([P, IN_F], F32, name="xf", tag="xf")
+                        x8 = xop.tile([P, IN_F], FP8, name="x8", tag="x8")
+                        nc.scalar.copy(out=xf[:], in_=xs[t][:])
+                        nc.sync.dma_start(out=out_0[t * P:(t + 1) * P, 0:IN_F], in_=xf[:])
+                        nc.scalar.activation(out=x8[:], in_=xf[:], func=ACT.Copy, scale=Y_SCALE, saturate=False)
+                        nc.sync.dma_start(out=out_1[t * P:(t + 1) * P, 0:IN_F], in_=x8[:].bitcast(U8))
 
-            s1c = xop.tile([P, NX], F32, name="s1c", tag="s1c")
+            s1c = [xop.tile([P, NX + 2], F32, name="s1c%d" % i, tag="s1c%d" % i) for i in range(2)]
             s2c = xop.tile([P, N], F32, name="s2c", tag="s2c")
-            nc.vector.tensor_copy(out=s1c[:], in_=s1[:])
-            nc.scalar.copy(out=s2c[:], in_=s2[:])
+            nc.vector.tensor_copy(out=s1c[0][:], in_=s1[0][:])
+            nc.scalar.copy(out=s1c[1][:], in_=s1[1][:])
+            nc.vector.tensor_copy(out=s2c[:], in_=s2[:])
 
             o0 = xop.tile([P, 2, J], F32, name="o0", tag="o0")
             o8 = xop.tile([P, 2, J], FP8, name="o8", tag="o8")
-            pt = psum.tile([P, 2, J], F32, name="pt", tag="b6")
+            pt = psum.tile([P, 2, J], F32, name="pt", tag="b0")
             for t in range(2):
-                parts = [rowsum[:, t * P:(t + 1) * P], colx[:, t * P:(t + 1) * P], s2c[:, t * P:(t + 1) * P], s1c[:, t * P:(t + 1) * P]]
+                parts = [rowsum[:, t * P:(t + 1) * P], colx[:, t * P:(t + 1) * P], s2c[:, t * P:(t + 1) * P],
+                         s1c[0][:, t * P:(t + 1) * P], s1c[1][:, t * P + 1:(t + 1) * P + 1]]
                 if t == 0:
-                    parts = parts + [colx[:, N:NX], s1c[:, N:NX]]
+                    parts = parts + [colx[:, N:NX], s1c[0][:, N:NX], s1c[1][:, N + 1:NX + 1]]
                 for i in range(len(parts)):
                     nc.tensor.matmul(out=pt[:, t, :], lhsT=parts[i], rhs=ident[:], is_transpose=True, start=(i == 0), stop=(i == len(parts) - 1))
             nc.vector.tensor_scalar(out=o0[:], in0=pt[:], scalar1=1.0, scalar2=None, op0=ALU.add)

@@ -25,10 +25,13 @@ RV = 8
 RB = 4
 CV = 640
 NX = N + P
+XP = 4
+SIDE_FIRST = 2
 TB = 12
 WARM_EVERY = 288
 WARM_FIRST = 32
 WARM_N = 4
+FIN_GAP = 12
 
 
 def build_program():
@@ -38,12 +41,14 @@ def build_program():
     banks = []
     open_bank = {"A": None, "B": None}
     made = []
-    state = {"row": 0, "pe": 0, "taken": 0}
+    state = {"row": 0, "pe": 0, "taken": 0, "fins": 0, "gap": 0}
+    fins = []
     cur = {"A": None, "B": None}
     left = {"A": NA, "B": NB}
     exp_due = {}
     fin_due = {}
     groups = []
+    side = [("wrap", i) for i in range(K // 2 + 1)] + [("xout", t, i) for t in range(2) for i in range(2 * XP)]
 
     def new_row(kind):
         if open_bank[kind] is None or open_bank[kind][1] == RB:
@@ -56,18 +61,29 @@ def build_program():
         left[kind] -= 1
         return len(rows) - 1
 
-    def make(kind, count, step):
+    def make(kind, count):
+        items = []
         for i in range(count):
             if cur[kind] is None:
-                if left[kind] == 0:
-                    return
                 cur[kind] = [new_row(kind), 0]
             rid, k = cur[kind]
-            prog.append(("abs" if kind == "A" else "ts", rid, k))
-            made.append((step, rid, k))
+            items.append(("abs" if kind == "A" else "ts", rid, k))
             cur[kind][1] += 1
             if cur[kind][1] == K:
                 cur[kind] = None
+        return items
+
+    def weave(first, second):
+        woven = []
+        total = len(first) + len(second)
+        taken = 0
+        for i in range(total):
+            if (taken + 1) * total <= (i + 1) * len(first):
+                woven.append(first[taken])
+                taken += 1
+            else:
+                woven.append(second[i - taken])
+        return woven
 
     def pe(item):
         prog.append(item)
@@ -85,24 +101,25 @@ def build_program():
             if k == 0:
                 groups.append(state["row"])
                 state["row"] += RV
-            for r in range(RV):
-                prog.append(("stt", g, k, r))
+            alone = [("stt", g, k, r) for r in range(RV)]
             if g >= 2 and k <= RV:
-                prog.append(("cadd", g - 2, k))
-            make("B", share(NB * K, step), step)
+                alone.append(("cadd", g - 2, k))
+            if SIDE_FIRST <= step < SIDE_FIRST + len(side):
+                alone.append(side[step - SIDE_FIRST])
+            vector = weave(alone, make("B", share(NB * K, step)))
+            scalar = make("A", share(NA * K, step))
             if g >= 1 and 1 <= k <= RV:
-                prog.append(("cexp", g - 1, k - 1))
-            make("A", share(NA * K, step), step)
-            if step == 2:
-                prog.append(("wrap",))
-            if step in (24, 48):
-                prog.append(("xout", step // 24 - 1))
+                scalar = [("cexp", g - 1, k - 1)] + scalar
+            for item in vector + scalar:
+                prog.append(item)
+                if item[0] == "ts" or item[0] == "abs":
+                    made.append((step, item[1], item[2]))
         for bank in exp_due.get(step, []):
             prog.append(("bexp", bank))
             fin_due.setdefault(step + 1, []).append(bank)
         for bank in fin_due.get(step, []):
             for q in range(RB):
-                pe(("fin", bank, q))
+                fins.append((bank, q))
         while state["taken"] < len(made) and made[state["taken"]][0] < step:
             st, rid, k = made[state["taken"]]
             state["taken"] += 1
@@ -112,6 +129,15 @@ def build_program():
             pe(("tp", rid, k))
             if k == K - 1 and q == RB - 1:
                 exp_due.setdefault(step + 1, []).append(bank)
+            state["gap"] += 1
+            if state["gap"] >= FIN_GAP and state["fins"] < len(fins):
+                pe(("fin", fins[state["fins"]][0], fins[state["fins"]][1]))
+                state["fins"] += 1
+                state["gap"] = 0
+        if step >= steps:
+            while state["fins"] < len(fins):
+                pe(("fin", fins[state["fins"]][0], fins[state["fins"]][1]))
+                state["fins"] += 1
     ng = len(groups)
     for r in range(RV):
         prog.append(("cexp", ng - 1, r))
@@ -261,6 +287,8 @@ def tile_minibatchdiscriminator_kernel(tc, tensor, T, out_0, out_1):
             ets = {}
             accs = {}
             es = {}
+            xfs = {}
+            x8s = {}
             with tc.manual_schedule(engines={mybir.EngineType.DVE, mybir.EngineType.PE, mybir.EngineType.Activation}):
                 for index in range(len(prog)):
                     item = prog[index]
@@ -332,17 +360,31 @@ def tile_minibatchdiscriminator_kernel(tc, tensor, T, out_0, out_1):
                             n = n0 + i - 1
                             nc.vector.tensor_tensor(out=colx[:, n + 1:n + 1 + P], in0=colx[:, n + 1:n + 1 + P], in1=es[g][:, i - 1, :], op=ALU.add)
                     elif what == "wrap":
-                        nc.scalar.copy(out=fsx[:, :, N:NX], in_=fsx[:, :, 0:P])
-                        nc.scalar.copy(out=snegx[:, N:NX], in_=snegx[:, 0:P])
+                        i = item[1]
+                        if i < K // 2:
+                            nc.vector.tensor_copy(out=fsx[:, 2 * i:2 * i + 2, N:NX], in_=fsx[:, 2 * i:2 * i + 2, 0:P])
+                        else:
+                            nc.vector.tensor_copy(out=snegx[:, N:NX], in_=snegx[:, 0:P])
                     else:
                         assert what == "xout"
-                        t = item[1]
-                        xf = xop.tile([P, IN_F], F32, name="xf", tag="xf")
-                        x8 = xop.tile([P, IN_F], FP8, name="x8", tag="x8")
-                        nc.scalar.copy(out=xf[:], in_=xs[t][:])
-                        nc.sync.dma_start(out=out_0[t * P:(t + 1) * P, 0:IN_F], in_=xf[:])
-                        nc.scalar.activation(out=x8[:], in_=xf[:], func=ACT.Copy, scale=Y_SCALE, saturate=False)
-                        nc.sync.dma_start(out=out_1[t * P:(t + 1) * P, 0:IN_F], in_=x8[:].bitcast(U8))
+                        t, i = item[1], item[2]
+                        width = IN_F // XP
+                        if i == 0:
+                            xf = xop.tile([P, IN_F], F32, name="xf", tag="xf")
+                            x8 = xop.tile([P, IN_F], FP8, name="x8", tag="x8")
+                            xfs[t] = xf
+                            x8s[t] = x8
+                        if i < XP:
+                            cols = slice(i * width, (i + 1) * width)
+                            nc.vector.tensor_copy(out=xfs[t][:, cols], in_=xs[t][:, cols])
+                            if i == XP - 1:
+                                nc.sync.dma_start(out=out_0[t * P:(t + 1) * P, 0:IN_F], in_=xfs[t][:])
+                        else:
+                            cols = slice((i - XP) * width, (i - XP + 1) * width)
+                            nc.vector.tensor_scalar(out=x8s[t][:, cols], in0=xfs[t][:, cols], scalar1=Y_SCALE, scalar2=None, op0=ALU.mult,
+                                                    saturate=False)
+                            if i == 2 * XP - 1:
+                                nc.sync.dma_start(out=out_1[t * P:(t + 1) * P, 0:IN_F], in_=x8s[t][:].bitcast(U8))
 
             s1c = [xop.tile([P, NX + 2], F32, name="s1c%d" % i, tag="s1c%d" % i) for i in range(2)]
             s2c = xop.tile([P, N], F32, name="s2c", tag="s2c")

@@ -18,8 +18,8 @@ ACT = mybir.ActivationFunctionType
 
 P = 128
 PASSES = 4
-NA = 100
-NB = 84
+NA = 104
+NB = 80
 NC = 72
 RV = 8
 RB = 4
@@ -28,9 +28,9 @@ NX = N + P
 XP = 4
 SIDE_FIRST = 2
 TB = 12
-WARM_EVERY = 288
+WARM_EVERY = 432
 WARM_FIRST = 32
-WARM_N = 4
+WARM_N = 3
 FIN_GAP = 12
 
 
@@ -160,9 +160,7 @@ def tile_minibatchdiscriminator_kernel(tc, tensor, T, out_0, out_1):
         colx = cst.tile([P, NX], F32, name="colx")
         snegx = cst.tile([P, NX], F32, name="snegx")
         ssum = cst.tile([P, N], F32, name="ssum")
-        half = cst.tile([P, 2, N], F32, name="half")
         fsx = cst.tile([P, K, NX], F32, name="fsx")
-        hneg = cst.tile([P, K, N], F32, name="hneg")
         zero = cst.tile([P, NX + 2], F32, name="zero")
         onesz = cst.tile([P, 1], F32, name="onesz")
         xs = [cst.tile([P, IN_F], BF16, name="xs%d" % t) for t in range(2)]
@@ -180,7 +178,6 @@ def tile_minibatchdiscriminator_kernel(tc, tensor, T, out_0, out_1):
         nc.gpsimd.memset(zero[:], 0.0)
         nc.vector.tensor_scalar(out=onesz[:], in0=ident[:, P - 1:P], scalar1=-1.0, scalar2=1.0, op0=ALU.mult, op1=ALU.add)
 
-        fp = []
         with ExitStack() as pre:
             rawp = pre.enter_context(tc.tile_pool(name="rawp", bufs=4))
             grpp = pre.enter_context(tc.tile_pool(name="grpp", bufs=3))
@@ -236,22 +233,20 @@ def tile_minibatchdiscriminator_kernel(tc, tensor, T, out_0, out_1):
                         nc.vector.tensor_copy(out=dst, in_=view)
                     else:
                         nc.scalar.copy(out=dst, in_=view)
+            sp = psum.tile([P, N], F32, name="sp", tag="b7")
             for b in range(8):
-                fpb = psum.tile([P, 2, N], F32, name="fp", tag="b%d" % b)
-                fp.append(fpb)
+                fpb = psum.tile([P, 2, N], F32, name="fp", tag="b%d" % (b % 7))
                 for kk in range(2):
                     for t in range(2):
                         nc.tensor.transpose(fpb[:, kk, t * P:(t + 1) * P], fnat[t][:, 2 * b + kk, :], ident[:])
-                nc.scalar.copy(out=fsx[:, 2 * b:2 * b + 2, 0:N], in_=fpb[:])
-                for kk in range(2):
-                    if b == 0:
-                        nc.vector.tensor_scalar(out=half[:, kk, :], in0=fpb[:, kk, :], scalar1=-0.5, scalar2=None, op0=ALU.mult)
-                    else:
-                        nc.vector.scalar_tensor_tensor(out=half[:, kk, :], in0=fpb[:, kk, :], scalar=-0.5, in1=half[:, kk, :],
-                                                       op0=ALU.mult, op1=ALU.add)
-        nc.vector.tensor_tensor(out=snegx[:, 0:N], in0=half[:, 0, :], in1=half[:, 1, :], op=ALU.add)
-        nc.scalar.activation(out=ssum[:], in_=snegx[:, 0:N], func=ACT.Copy, scale=-2.0)
-        nc.vector.tensor_scalar(out=hneg[:], in0=fsx[:, :, 0:N], scalar1=-0.5, scalar2=None, op0=ALU.mult)
+                        nc.tensor.matmul(out=sp[:, t * P:(t + 1) * P], lhsT=fnat[t][:, 2 * b + kk, :], rhs=ident[:], is_transpose=True,
+                                         start=(b == 0 and kk == 0 and t == 0), stop=(b == 7 and kk == 1 and t == 1))
+                if b % 2 == 0:
+                    nc.scalar.copy(out=fsx[:, 2 * b:2 * b + 2, 0:N], in_=fpb[:])
+                else:
+                    nc.vector.tensor_copy(out=fsx[:, 2 * b:2 * b + 2, 0:N], in_=fpb[:])
+            nc.vector.tensor_scalar(out=snegx[:, 0:N], in0=sp[:], scalar1=-0.5, scalar2=None, op0=ALU.mult)
+            nc.scalar.copy(out=ssum[:], in_=sp[:])
 
         with ExitStack() as mainctx:
             tpool = mainctx.enter_context(tc.tile_pool(name="tpool", bufs=TB))
@@ -302,9 +297,12 @@ def tile_minibatchdiscriminator_kernel(tc, tensor, T, out_0, out_1):
                         if what == "abs":
                             nc.scalar.activation(out=terms[rid][:, k, :], in_=fsx[:, k, n + 1:n + 1 + P], func=ACT.Abs, scale=-1.0,
                                                  bias=fsx[:, k, n:n + 1])
+                        elif k == 0:
+                            nc.vector.tensor_scalar(out=terms[rid][:, k, :], in0=fsx[:, k, n + 1:n + 1 + P], scalar1=fsx[:, k, n:n + 1],
+                                                    scalar2=snegx[:, n:n + 1], op0=ALU.max, op1=ALU.add)
                         else:
                             nc.vector.tensor_scalar(out=terms[rid][:, k, :], in0=fsx[:, k, n + 1:n + 1 + P], scalar1=fsx[:, k, n:n + 1],
-                                                    scalar2=hneg[:, k, n:n + 1], op0=ALU.max, op1=ALU.add)
+                                                    scalar2=None, op0=ALU.max)
                     elif what == "tp":
                         rid, k = item[1], item[2]
                         kind, n, bank, q = rows[rid]

@@ -23,11 +23,11 @@ NB = 80
 NC = 72
 RV = 8
 RB = 4
-CV = 640
+CV = 512
 NX = N + P
 XP = 4
-SIDE_FIRST = 2
-TB = 12
+SIDE_FIRST = 40
+TB = 14
 WARM_EVERY = 432
 WARM_FIRST = 32
 WARM_N = 3

@@ -28,9 +28,10 @@ NX = N + P
 XP = 4
 SIDE_FIRST = 40
 TB = 14
-WARM_EVERY = 432
+WARM_EVERY = 864
 WARM_FIRST = 32
 WARM_N = 3
+LAG = 1
 FIN_GAP = 12
 
 
@@ -95,7 +96,7 @@ def build_program():
     def share(total, step):
         return (step + 1) * total // steps - step * total // steps
 
-    for step in range(steps + 6):
+    for step in range(steps + 6 * LAG):
         if step < steps:
             g, k = divmod(step, K)
             if k == 0:
@@ -116,11 +117,11 @@ def build_program():
                     made.append((step, item[1], item[2]))
         for bank in exp_due.get(step, []):
             prog.append(("bexp", bank))
-            fin_due.setdefault(step + 1, []).append(bank)
+            fin_due.setdefault(step + LAG, []).append(bank)
         for bank in fin_due.get(step, []):
             for q in range(RB):
                 fins.append((bank, q))
-        while state["taken"] < len(made) and made[state["taken"]][0] < step:
+        while state["taken"] < len(made) and made[state["taken"]][0] + LAG <= step:
             st, rid, k = made[state["taken"]]
             state["taken"] += 1
             kind, n, bank, q = rows[rid]
@@ -128,7 +129,7 @@ def build_program():
                 pe(("tp", rid, -1))
             pe(("tp", rid, k))
             if k == K - 1 and q == RB - 1:
-                exp_due.setdefault(step + 1, []).append(bank)
+                exp_due.setdefault(step + LAG, []).append(bank)
             state["gap"] += 1
             if state["gap"] >= FIN_GAP and state["fins"] < len(fins):
                 pe(("fin", fins[state["fins"]][0], fins[state["fins"]][1]))
@@ -145,7 +146,7 @@ def build_program():
         for i in range(RV + 1):
             prog.append(("cadd", g, i))
     assert state["row"] == N and state["taken"] == len(made) == (NA + NB) * K
-    assert max(fin_due) < steps + 6
+    assert max(fin_due) < steps + 6 * LAG
     return prog, rows, banks, groups
 
 
@@ -179,7 +180,7 @@ def tile_minibatchdiscriminator_kernel(tc, tensor, T, out_0, out_1):
         nc.vector.tensor_scalar(out=onesz[:], in0=ident[:, P - 1:P], scalar1=-1.0, scalar2=1.0, op0=ALU.mult, op1=ALU.add)
 
         with ExitStack() as pre:
-            rawp = pre.enter_context(tc.tile_pool(name="rawp", bufs=4))
+            rawp = pre.enter_context(tc.tile_pool(name="rawp", bufs=8))
             grpp = pre.enter_context(tc.tile_pool(name="grpp", bufs=3))
             keep = pre.enter_context(tc.tile_pool(name="keep", bufs=1))
             tqs = [tq0] + [keep.tile([P, 1024], U32, name="tq%d" % i, align_bytes=64) for i in range(1, 2 * PASSES)]

@@ -170,9 +170,6 @@ def tile_minibatchdiscriminator_kernel(tc, tensor, T, out_0, out_1):
         tq0 = cst.tile([P, 1024], U32, name="tq0", align_bytes=64)
         tsc0 = cst.tile([P, 1024], U8, name="tsc0", align_bytes=64)
 
-        for t in range(2):
-            nc.sync.dma_start(out=xs[t][:], in_=tensor[t * P:(t + 1) * P, :])
-
         make_identity(nc, ident[:])
         nc.gpsimd.memset(rowsum[:], 0.0)
         nc.gpsimd.memset(colx[:], 0.0)
@@ -189,12 +186,30 @@ def tile_minibatchdiscriminator_kernel(tc, tensor, T, out_0, out_1):
             fnat = [keep.tile([P, K, J], F32, name="fnat%d" % t) for t in range(2)]
 
             tv = T.rearrange("(s p t) j k -> s p t (j k)", p=P, t=4)
+            pieces = [(0, 0, 0, 512), (0, 0, 512, 512)] + [(s, h, 0, 1024) for s in range(PASSES) for h in range(2)][1:]
             raws = []
-            for s in range(PASSES):
-                for h in range(2):
-                    raw = rawp.tile([P, 4, 1024], BF16, name="raw", tag="raw")
-                    nc.sync.dma_start(out=raw[:], in_=tv[s][:, :, h * 1024:(h + 1) * 1024])
-                    raws.append(raw)
+            for index in range(len(pieces)):
+                s, h, c0, width = pieces[index]
+                raw = rawp.tile([P, 4, width], BF16, name="raw", tag="raw")
+                nc.sync.dma_start(out=raw[:], in_=tv[s][:, :, h * 1024 + c0:h * 1024 + c0 + width])
+                raws.append(raw)
+                if index == 1:
+                    for t in range(2):
+                        nc.sync.dma_start(out=xs[t][:], in_=tensor[t * P:(t + 1) * P, :])
+
+            def prepare(index):
+                s, h, c0, width = pieces[index]
+                cv = width * CV // 1024
+                grp = grpp.tile([P, width, 4], BF16, name="grp", tag="grp", align_bytes=64)
+                nc.vector.tensor_copy(out=grp[:, 0:cv, :].rearrange("p (c i) t -> p c t i", i=4),
+                                      in_=raws[index][:, :, 0:cv].rearrange("p t (c i) -> p c t i", i=4))
+                nc.scalar.copy(out=grp[:, cv:width, :].rearrange("p (c i) t -> p c t i", i=4),
+                               in_=raws[index][:, :, cv:width].rearrange("p t (c i) -> p c t i", i=4))
+                nc.vector.quantize_mx(out=tqs[2 * s + h][:, c0:c0 + width].bitcast(FP8X4), scales=tscs[2 * s + h][:, c0:c0 + width],
+                                      in_=grp[:].rearrange("p c t -> p (c t)"))
+
+            prepare(0)
+            prepare(1)
 
             for g in range(PASSES):
                 xt = psum.tile([P, 2, N], F32, name="xt", tag="b%d" % g)
@@ -206,26 +221,21 @@ def tile_minibatchdiscriminator_kernel(tc, tensor, T, out_0, out_1):
             nc.vector.quantize_mx(out=xq[:].bitcast(FP8X4), scales=xsc[:], in_=xg[:].rearrange("p g n f -> p (g n f)"))
 
             ft = [psum.tile([P, 512], F32, name="ft", tag="b%d" % b) for b in range(8)]
-            for s in range(PASSES):
-                for h in range(2):
-                    grp = grpp.tile([P, 1024, 4], BF16, name="grp", tag="grp", align_bytes=64)
-                    src = raws[2 * s + h][:].rearrange("p t c -> p c t")
-                    nc.vector.tensor_copy(out=grp[:, 0:CV, :], in_=src[:, 0:CV, :])
-                    nc.scalar.copy(out=grp[:, CV:1024, :], in_=src[:, CV:1024, :])
-                    tq = tqs[2 * s + h]
-                    tsc = tscs[2 * s + h]
-                    nc.vector.quantize_mx(out=tq[:].bitcast(FP8X4), scales=tsc[:], in_=grp[:].rearrange("p c t -> p (c t)"))
-                    for w in range(2):
-                        for t in range(2):
-                            nc.tensor.matmul_mx(
-                                out=ft[4 * t + 2 * h + w][:],
-                                lhsT=xq[:, s * N + t * P:s * N + (t + 1) * P].bitcast(FP8X4),
-                                lhsT_scale=xsc[:, s * N + t * P:s * N + (t + 1) * P],
-                                rhs=tq[:, 512 * w:512 * (w + 1)].bitcast(FP8X4),
-                                rhs_scale=tsc[:, 512 * w:512 * (w + 1)],
-                                start=(s == 0),
-                                stop=(s == PASSES - 1),
-                            )
+            for index in range(len(pieces)):
+                s, h, c0, width = pieces[index]
+                if index > 1:
+                    prepare(index)
+                for w in range(c0 // 512, (c0 + width) // 512):
+                    for t in range(2):
+                        nc.tensor.matmul_mx(
+                            out=ft[4 * t + 2 * h + w][:],
+                            lhsT=xq[:, s * N + t * P:s * N + (t + 1) * P].bitcast(FP8X4),
+                            lhsT_scale=xsc[:, s * N + t * P:s * N + (t + 1) * P],
+                            rhs=tqs[2 * s + h][:, 512 * w:512 * (w + 1)].bitcast(FP8X4),
+                            rhs_scale=tscs[2 * s + h][:, 512 * w:512 * (w + 1)],
+                            start=(s == 0),
+                            stop=(s == PASSES - 1),
+                        )
             for w in range(4):
                 for t in range(2):
                     dst = fnat[t][:, :, 32 * w:32 * (w + 1)]

@@ -23,41 +23,56 @@ NB = 80
 NC = 72
 RV = 8
 RB = 4
+SINGLE = 0
 CV = 512
 NX = N + P
 XP = 4
-SIDE_FIRST = 40
+LEAD = 2
+XH1 = 8
+XH2 = 3
+NDUMMY = 14
+NDUMMY2 = 1
+IDLE_HEAD = 3
+A_EARLY = 0
+B_EARLY = 0
 TB = 14
+EB = 8
+FIN_LAG = 2
 WARM_EVERY = 864
-WARM_FIRST = 32
+WARM_FIRST = 64
 WARM_N = 3
 LAG = 1
+B_STT = 0
 FIN_GAP = 12
 
 
 def build_program():
     prog = []
-    steps = (NC // RV) * K
+    c_steps = (NC // RV) * K
+    steps = LEAD + c_steps
+    a_steps = steps - A_EARLY
+    b_steps = c_steps - B_EARLY
     rows = []
     banks = []
     open_bank = {"A": None, "B": None}
     made = []
-    state = {"row": 0, "pe": 0, "taken": 0, "fins": 0, "gap": 0}
+    state = {"row": 0, "pe": 0, "taken": 0, "fins": 0, "gap": 0, "open": 0}
     fins = []
     cur = {"A": None, "B": None}
     left = {"A": NA, "B": NB}
     exp_due = {}
     fin_due = {}
     groups = []
-    side = [("wrap", i) for i in range(K // 2 + 1)] + [("xout", t, i) for t in range(2) for i in range(2 * XP)]
+    side = [("xout", t, i) for t in range(2) for i in range(2 * XP)][XH1 + XH2:] + [("wrap", i) for i in range(K // 2)] + [("sneg",), ("wrap", K // 2)]
 
     def new_row(kind):
-        if open_bank[kind] is None or open_bank[kind][1] == RB:
-            banks.append(kind)
+        if open_bank[kind] is None or open_bank[kind][1] == banks[open_bank[kind][0]][1]:
+            banks.append((kind, RB if left[kind] > SINGLE else 1))
             open_bank[kind] = [len(banks) - 1, 0]
         bank, q = open_bank[kind]
         open_bank[kind][1] += 1
-        rows.append((kind, state["row"], bank, q))
+        done = NB - left["B"]
+        rows.append((kind, state["row"], bank, q, kind == "B" and (done + 1) * B_STT // NB == done * B_STT // NB))
         state["row"] += 1
         left[kind] -= 1
         return len(rows) - 1
@@ -93,67 +108,84 @@ def build_program():
             for i in range(WARM_N):
                 prog.append(("warm",))
 
-    def share(total, step):
-        return (step + 1) * total // steps - step * total // steps
+    def fin_one():
+        pe(("fin", fins[state["fins"]][0], fins[state["fins"]][1]))
+        state["fins"] += 1
+        state["gap"] = 0
 
-    for step in range(steps + 6 * LAG):
-        if step < steps:
-            g, k = divmod(step, K)
+    def share(total, step, over):
+        return (step + 1) * total // over - step * total // over
+
+    ng = NC // RV
+    step = 0
+    while step < steps or state["taken"] < len(made) or state["open"] > 0 or state["fins"] < len(fins):
+        vector = []
+        scalar = []
+        if step < LEAD:
+            first = step * len(side) // LEAD
+            vector = side[first:(step + 1) * len(side) // LEAD]
+            if step == LEAD - 1:
+                scalar.append(("ssum",))
+        cs = step - LEAD
+        if 0 <= cs < c_steps:
+            g, k = divmod(cs, K)
             if k == 0:
                 groups.append(state["row"])
                 state["row"] += RV
             alone = [("stt", g, k, r) for r in range(RV)]
-            if g >= 2 and k <= RV:
-                alone.append(("cadd", g - 2, k))
-            if SIDE_FIRST <= step < SIDE_FIRST + len(side):
-                alone.append(side[step - SIDE_FIRST])
-            vector = weave(alone, make("B", share(NB * K, step)))
-            scalar = make("A", share(NA * K, step))
-            if g >= 1 and 1 <= k <= RV:
-                scalar = [("cexp", g - 1, k - 1)] + scalar
-            for item in vector + scalar:
-                prog.append(item)
-                if item[0] == "ts" or item[0] == "abs":
-                    made.append((step, item[1], item[2]))
+            if g >= 1 and 2 <= k < RV + 2:
+                alone.append(("cadd", g - 1, k - 1))
+            if g >= 1 and k == RV + 2:
+                alone.append(("cadd", g - 1, 0))
+            vector = weave(alone, make("B", share(NB * K, cs, b_steps)) if cs < b_steps else [])
+            if g >= 1 and k < RV:
+                scalar.append(("cexp", g - 1, k))
+        if cs == c_steps:
+            for r in range(RV):
+                vector.append(("cexp", ng - 1, r))
+                vector.append(("cadd", ng - 1, r + 1))
+            vector.append(("cadd", ng - 1, 0))
+        if step < a_steps:
+            scalar = scalar + make("A", share(NA * K, step, a_steps))
+        for item in vector + scalar:
+            prog.append(item)
+        for item in scalar + vector:
+            if item[0] == "ts" or item[0] == "abs":
+                made.append((step, item[1], item[2]))
         for bank in exp_due.get(step, []):
             prog.append(("bexp", bank))
-            fin_due.setdefault(step + LAG, []).append(bank)
+            fin_due.setdefault(step + FIN_LAG, []).append(bank)
         for bank in fin_due.get(step, []):
-            for q in range(RB):
+            state["open"] -= 1
+            for q in range(banks[bank][1]):
                 fins.append((bank, q))
         while state["taken"] < len(made) and made[state["taken"]][0] + LAG <= step:
             st, rid, k = made[state["taken"]]
             state["taken"] += 1
-            kind, n, bank, q = rows[rid]
-            if kind == "B" and k == 0:
+            kind, n, bank, q, opened = rows[rid]
+            if opened and k == 0:
                 pe(("tp", rid, -1))
             pe(("tp", rid, k))
-            if k == K - 1 and q == RB - 1:
+            if k == K - 1 and q == banks[bank][1] - 1:
                 exp_due.setdefault(step + LAG, []).append(bank)
+                state["open"] += 1
             state["gap"] += 1
             if state["gap"] >= FIN_GAP and state["fins"] < len(fins):
-                pe(("fin", fins[state["fins"]][0], fins[state["fins"]][1]))
-                state["fins"] += 1
-                state["gap"] = 0
-        if step >= steps:
+                fin_one()
+        if step >= steps - 1:
             while state["fins"] < len(fins):
-                pe(("fin", fins[state["fins"]][0], fins[state["fins"]][1]))
-                state["fins"] += 1
-    ng = len(groups)
-    for r in range(RV):
-        prog.append(("cexp", ng - 1, r))
-    for g in (ng - 2, ng - 1):
-        for i in range(RV + 1):
-            prog.append(("cadd", g, i))
+                fin_one()
+        step += 1
     assert state["row"] == N and state["taken"] == len(made) == (NA + NB) * K
-    assert max(fin_due) < steps + 6 * LAG
     return prog, rows, banks, groups
 
 
 def tile_minibatchdiscriminator_kernel(tc, tensor, T, out_0, out_1):
     nc = tc.nc
+    pinned = {mybir.EngineType.DVE, mybir.EngineType.PE, mybir.EngineType.Activation}
     with ExitStack() as ctx:
         cst = ctx.enter_context(tc.tile_pool(name="cst", bufs=1))
+        xop = ctx.enter_context(tc.tile_pool(name="xop", bufs=2))
         psum = ctx.enter_context(tc.psum_pool(name="psum", bufs=1))
 
         ident = cst.tile([P, P], F32, name="ident")
@@ -162,7 +194,7 @@ def tile_minibatchdiscriminator_kernel(tc, tensor, T, out_0, out_1):
         snegx = cst.tile([P, NX], F32, name="snegx")
         ssum = cst.tile([P, N], F32, name="ssum")
         fsx = cst.tile([P, K, NX], F32, name="fsx")
-        zero = cst.tile([P, NX + 2], F32, name="zero")
+        zero = cst.tile([P, P], F32, name="zero")
         onesz = cst.tile([P, 1], F32, name="onesz")
         xs = [cst.tile([P, IN_F], BF16, name="xs%d" % t) for t in range(2)]
         xq = cst.tile([P, PASSES * N], U32, name="xq", align_bytes=64)
@@ -172,9 +204,32 @@ def tile_minibatchdiscriminator_kernel(tc, tensor, T, out_0, out_1):
 
         make_identity(nc, ident[:])
         nc.gpsimd.memset(rowsum[:], 0.0)
-        nc.gpsimd.memset(colx[:], 0.0)
+        nc.gpsimd.memset(colx[:, 0:N], 1.0)
+        nc.gpsimd.memset(colx[:, N:NX], 0.0)
         nc.gpsimd.memset(zero[:], 0.0)
         nc.vector.tensor_scalar(out=onesz[:], in0=ident[:, P - 1:P], scalar1=-1.0, scalar2=1.0, op0=ALU.mult, op1=ALU.add)
+
+        xfs = {}
+        x8s = {}
+
+        def xout(t, i):
+            width = IN_F // XP
+            if i == 0:
+                xf = xop.tile([P, IN_F], F32, name="xf", tag="xf")
+                x8 = xop.tile([P, IN_F], FP8, name="x8", tag="x8")
+                xfs[t] = xf
+                x8s[t] = x8
+            if i < XP:
+                cols = slice(i * width, (i + 1) * width)
+                nc.vector.tensor_copy(out=xfs[t][:, cols], in_=xs[t][:, cols])
+                if i == XP - 1:
+                    nc.sync.dma_start(out=out_0[t * P:(t + 1) * P, 0:IN_F], in_=xfs[t][:])
+            else:
+                cols = slice((i - XP) * width, (i - XP + 1) * width)
+                nc.vector.tensor_scalar(out=x8s[t][:, cols], in0=xfs[t][:, cols], scalar1=Y_SCALE, scalar2=None, op0=ALU.mult,
+                                        saturate=False)
+                if i == 2 * XP - 1:
+                    nc.sync.dma_start(out=out_1[t * P:(t + 1) * P, 0:IN_F], in_=x8s[t][:].bitcast(U8))
 
         with ExitStack() as pre:
             rawp = pre.enter_context(tc.tile_pool(name="rawp", bufs=8))
@@ -197,38 +252,31 @@ def tile_minibatchdiscriminator_kernel(tc, tensor, T, out_0, out_1):
                     for t in range(2):
                         nc.sync.dma_start(out=xs[t][:], in_=tensor[t * P:(t + 1) * P, :])
 
-            def prepare(index):
+            grps = {}
+
+            def interleave(index):
                 s, h, c0, width = pieces[index]
                 cv = width * CV // 1024
                 grp = grpp.tile([P, width, 4], BF16, name="grp", tag="grp", align_bytes=64)
+                grps[index] = grp
                 nc.vector.tensor_copy(out=grp[:, 0:cv, :].rearrange("p (c i) t -> p c t i", i=4),
                                       in_=raws[index][:, :, 0:cv].rearrange("p t (c i) -> p c t i", i=4))
                 nc.scalar.copy(out=grp[:, cv:width, :].rearrange("p (c i) t -> p c t i", i=4),
                                in_=raws[index][:, :, cv:width].rearrange("p t (c i) -> p c t i", i=4))
-                nc.vector.quantize_mx(out=tqs[2 * s + h][:, c0:c0 + width].bitcast(FP8X4), scales=tscs[2 * s + h][:, c0:c0 + width],
-                                      in_=grp[:].rearrange("p c t -> p (c t)"))
 
-            prepare(0)
-            prepare(1)
-
-            for g in range(PASSES):
-                xt = psum.tile([P, 2, N], F32, name="xt", tag="b%d" % g)
-                for t in range(2):
-                    words = xs[t][:].bitcast(F32)
-                    for u in range(2):
-                        nc.tensor.transpose(xt[:, u, t * P:(t + 1) * P], words[:, 256 * g + u:256 * (g + 1):2], ident[:])
-                nc.vector.tensor_copy(out=xg[:, g, :, :].bitcast(F32), in_=xt[:].rearrange("p u n -> p n u"))
-            nc.vector.quantize_mx(out=xq[:].bitcast(FP8X4), scales=xsc[:], in_=xg[:].rearrange("p g n f -> p (g n f)"))
-
-            ft = [psum.tile([P, 512], F32, name="ft", tag="b%d" % b) for b in range(8)]
-            for index in range(len(pieces)):
+            def quantise(index):
                 s, h, c0, width = pieces[index]
-                if index > 1:
-                    prepare(index)
+                nc.vector.quantize_mx(out=tqs[2 * s + h][:, c0:c0 + width].bitcast(FP8X4), scales=tscs[2 * s + h][:, c0:c0 + width],
+                                      in_=grps[index][:].rearrange("p c t -> p (c t)"))
+
+            fts = []
+
+            def multiply(index):
+                s, h, c0, width = pieces[index]
                 for w in range(c0 // 512, (c0 + width) // 512):
                     for t in range(2):
                         nc.tensor.matmul_mx(
-                            out=ft[4 * t + 2 * h + w][:],
+                            out=fts[4 * t + 2 * h + w][:],
                             lhsT=xq[:, s * N + t * P:s * N + (t + 1) * P].bitcast(FP8X4),
                             lhsT_scale=xsc[:, s * N + t * P:s * N + (t + 1) * P],
                             rhs=tqs[2 * s + h][:, 512 * w:512 * (w + 1)].bitcast(FP8X4),
@@ -236,66 +284,104 @@ def tile_minibatchdiscriminator_kernel(tc, tensor, T, out_0, out_1):
                             start=(s == 0),
                             stop=(s == PASSES - 1),
                         )
-            for w in range(4):
-                for t in range(2):
-                    dst = fnat[t][:, :, 32 * w:32 * (w + 1)]
-                    view = ft[4 * t + w][:].rearrange("p (j k) -> p k j", k=K)
-                    if t == 0:
-                        nc.vector.tensor_copy(out=dst, in_=view)
-                    else:
-                        nc.scalar.copy(out=dst, in_=view)
-            sp = psum.tile([P, N], F32, name="sp", tag="b7")
-            for b in range(8):
-                fpb = psum.tile([P, 2, N], F32, name="fp", tag="b%d" % (b % 7))
-                for kk in range(2):
+
+            with tc.manual_schedule(engines=pinned):
+                wu = psum.tile([P, P], F32, name="wu", tag="b7")
+                for d in range(NDUMMY):
+                    nc.tensor.matmul(out=wu[:], lhsT=ident[:], rhs=ident[:], start=True, stop=True)
+                interleave(0)
+                interleave(1)
+                quantise(0)
+                quantise(1)
+                for piece in range(XH1):
+                    xout(piece // (2 * XP), piece % (2 * XP))
+                for g in range(PASSES):
+                    xt = psum.tile([P, 2, N], F32, name="xt", tag="b%d" % g)
                     for t in range(2):
-                        nc.tensor.transpose(fpb[:, kk, t * P:(t + 1) * P], fnat[t][:, 2 * b + kk, :], ident[:])
-                        nc.tensor.matmul(out=sp[:, t * P:(t + 1) * P], lhsT=fnat[t][:, 2 * b + kk, :], rhs=ident[:], is_transpose=True,
-                                         start=(b == 0 and kk == 0 and t == 0), stop=(b == 7 and kk == 1 and t == 1))
-                if b % 2 == 0:
-                    nc.scalar.copy(out=fsx[:, 2 * b:2 * b + 2, 0:N], in_=fpb[:])
-                else:
-                    nc.vector.tensor_copy(out=fsx[:, 2 * b:2 * b + 2, 0:N], in_=fpb[:])
-            nc.vector.tensor_scalar(out=snegx[:, 0:N], in0=sp[:], scalar1=-0.5, scalar2=None, op0=ALU.mult)
-            nc.scalar.copy(out=ssum[:], in_=sp[:])
+                        words = xs[t][:].bitcast(F32)
+                        for u in range(2):
+                            nc.tensor.transpose(xt[:, u, t * P:(t + 1) * P], words[:, 256 * g + u:256 * (g + 1):2], ident[:])
+                    if g < NDUMMY2:
+                        nc.tensor.matmul(out=wu[:], lhsT=ident[:], rhs=ident[:], start=True, stop=True)
+                    nc.scalar.copy(out=xg[:, g, :, :].bitcast(F32), in_=xt[:].rearrange("p u n -> p n u"))
+                interleave(2)
+                nc.vector.quantize_mx(out=xq[:].bitcast(FP8X4), scales=xsc[:], in_=xg[:].rearrange("p g n f -> p (g n f)"))
+                for b in range(8):
+                    ft = psum.tile([P, 512], F32, name="ft", tag="b%d" % b)
+                    fts.append(ft)
+                multiply(0)
+                multiply(1)
+                for index in range(2, len(pieces)):
+                    if index + 1 < len(pieces):
+                        interleave(index + 1)
+                    quantise(index)
+                    multiply(index)
+                for w in range(4):
+                    for t in range(2):
+                        dst = fnat[t][:, :, 32 * w:32 * (w + 1)]
+                        view = fts[4 * t + w][:].rearrange("p (j k) -> p k j", k=K)
+                        if t == 0 and w != 0:
+                            nc.vector.tensor_copy(out=dst, in_=view)
+                        else:
+                            nc.scalar.copy(out=dst, in_=view)
+                idleh = psum.tile([P, 512], F32, name="idleh", tag="b0")
+                for i in range(IDLE_HEAD):
+                    nc.tensor.matmul_mx(out=idleh[:], lhsT=xq[:, 0:P].bitcast(FP8X4), lhsT_scale=xsc[:, 0:P],
+                                        rhs=tq0[:, 0:512].bitcast(FP8X4), rhs_scale=tsc0[:, 0:512], start=True, stop=True)
+                for piece in range(XH1, XH1 + XH2):
+                    xout(piece // (2 * XP), piece % (2 * XP))
+                for b in range(8):
+                    fpb = psum.tile([P, 2, N], F32, name="fp", tag="b%d" % (b % 7))
+                    for kk in range(2):
+                        for t in range(2):
+                            nc.tensor.transpose(fpb[:, kk, t * P:(t + 1) * P], fnat[t][:, 2 * b + kk, :], ident[:])
+                    if b % 2 == 0:
+                        nc.scalar.copy(out=fsx[:, 2 * b:2 * b + 2, 0:N], in_=fpb[:])
+                    else:
+                        nc.vector.tensor_copy(out=fsx[:, 2 * b:2 * b + 2, 0:N], in_=fpb[:])
+                sp = psum.tile([P, N], F32, name="sp", tag="b7")
+                for k in range(K):
+                    for t in range(2):
+                        nc.tensor.matmul(out=sp[:, t * P:(t + 1) * P], lhsT=fnat[t][:, k, :], rhs=ident[:], is_transpose=True,
+                                         start=(k == 0 and t == 0), stop=(k == K - 1 and t == 1))
 
         with ExitStack() as mainctx:
             tpool = mainctx.enter_context(tc.tile_pool(name="tpool", bufs=TB))
-            epool = mainctx.enter_context(tc.tile_pool(name="epool", bufs=4))
+            epool = mainctx.enter_context(tc.tile_pool(name="epool", bufs=EB))
             accp = mainctx.enter_context(tc.tile_pool(name="accp", bufs=3))
-            xop = mainctx.enter_context(tc.tile_pool(name="xop", bufs=2))
-
-            s1 = [psum.tile([P, NX + 2], F32, name="s1", tag="b%d" % (4 + i)) for i in range(2)]
-            s2 = psum.tile([P, N], F32, name="s2", tag="b6")
-            idle = psum.tile([P, 512], F32, name="idle", tag="b7")
-            for i in range(2):
-                nc.tensor.matmul(out=s1[i][:], lhsT=zero[:, 0:P], rhs=zero[:], start=True, stop=False)
-            nc.tensor.matmul(out=s2[:], lhsT=zero[:, 0:P], rhs=zero[:, 0:N], start=True, stop=False)
+            endp = mainctx.enter_context(tc.tile_pool(name="endp", bufs=1))
 
             prog, rows, banks, groups = build_program()
             last_fin = {}
+            row_of = {}
+            for rid in range(len(rows)):
+                row_of[(rows[rid][2], rows[rid][3])] = rid
             for index in range(len(prog)):
                 if prog[index][0] == "fin":
-                    rid = [r for r in range(len(rows)) if rows[r][2] == prog[index][1] and rows[r][3] == prog[index][2]][0]
+                    rid = row_of[(prog[index][1], prog[index][2])]
                     last_fin[(rows[rid][1] + 1) % 2] = index
                     last_fin[2] = index
             bank_count = {"A": 0, "B": 0}
             bank_tag = []
-            for kind in banks:
+            for kind, size in banks:
                 bank_tag.append("b%d" % ((0 if kind == "A" else 2) + bank_count[kind] % 2))
                 bank_count[kind] += 1
-            row_of = {}
-            for rid in range(len(rows)):
-                row_of[(rows[rid][2], rows[rid][3])] = rid
 
+            s1c = [endp.tile([P, NX + 2], F32, name="s1c%d" % i) for i in range(2)]
+            s2c = endp.tile([P, N], F32, name="s2c")
             terms = {}
             lts = {}
             ets = {}
             accs = {}
             es = {}
-            xfs = {}
-            x8s = {}
-            with tc.manual_schedule(engines={mybir.EngineType.DVE, mybir.EngineType.PE, mybir.EngineType.Activation}):
+            idles = []
+            with tc.manual_schedule(engines=pinned):
+                s1 = [psum.tile([P, 512], F32, name="s1", tag="b%d" % (4 + i)) for i in range(2)]
+                s2 = psum.tile([P, N], F32, name="s2", tag="b6")
+                for acc0, width in ((s1[0], 512), (s1[1], 512), (s2, N)):
+                    for c in range(width // P):
+                        nc.tensor.matmul(out=acc0[:, c * P:(c + 1) * P], lhsT=zero[:], rhs=ident[:], is_transpose=True, start=(c == 0), stop=False)
+
                 for index in range(len(prog)):
                     item = prog[index]
                     what = item[0]
@@ -308,7 +394,10 @@ def tile_minibatchdiscriminator_kernel(tc, tensor, T, out_0, out_1):
                         if what == "abs":
                             nc.scalar.activation(out=terms[rid][:, k, :], in_=fsx[:, k, n + 1:n + 1 + P], func=ACT.Abs, scale=-1.0,
                                                  bias=fsx[:, k, n:n + 1])
-                        elif k == 0:
+                        elif k == 0 and not rows[rid][4]:
+                            nc.vector.scalar_tensor_tensor(out=terms[rid][:, k, :], in0=fsx[:, k, n + 1:n + 1 + P], scalar=fsx[:, k, n:n + 1],
+                                                           in1=snegx[:, n + 1:n + 1 + P], op0=ALU.max, op1=ALU.add)
+                        elif k == (0 if rows[rid][4] else 1):
                             nc.vector.tensor_scalar(out=terms[rid][:, k, :], in0=fsx[:, k, n + 1:n + 1 + P], scalar1=fsx[:, k, n:n + 1],
                                                     scalar2=snegx[:, n:n + 1], op0=ALU.max, op1=ALU.add)
                         else:
@@ -316,18 +405,19 @@ def tile_minibatchdiscriminator_kernel(tc, tensor, T, out_0, out_1):
                                                     scalar2=None, op0=ALU.max)
                     elif what == "tp":
                         rid, k = item[1], item[2]
-                        kind, n, bank, q = rows[rid]
-                        first = (k == -1) if kind == "B" else (k == 0)
+                        kind, n, bank, q, opened = rows[rid]
+                        first = (k == -1) if opened else (k == 0)
                         if first and q == 0:
                             lt = psum.tile([P, RB, P], F32, name="lt", tag=bank_tag[bank])
                             lts[bank] = lt
-                        nc.tensor.matmul(out=lts[bank][:, q, :], lhsT=(snegx[:, n + 1:n + 1 + P] if k == -1 else terms[rid][:, k, :]),
-                                         rhs=ident[:], is_transpose=True, start=first, stop=(k == K - 1))
+                        nc.tensor.matmul(out=lts[bank][:, q, :], lhsT=(snegx[:, n + 1:n + 1 + P] if k == -1 else terms[rid][:, k, :]), rhs=ident[:],
+                                         is_transpose=True, start=first, stop=(k == K - 1))
                     elif what == "bexp":
                         bank = item[1]
+                        kind, size = banks[bank]
                         et = epool.tile([P, RB, P], F32, name="et", tag="et")
                         ets[bank] = et
-                        nc.scalar.activation(out=et[:], in_=lts[bank][:], func=ACT.Exp, scale=(-1.0 if banks[bank] == "A" else -2.0))
+                        nc.scalar.activation(out=et[:, 0:size, :], in_=lts[bank][:, 0:size, :], func=ACT.Exp, scale=(-1.0 if kind == "A" else -2.0))
                     elif what == "fin":
                         bank, q = item[1], item[2]
                         n = rows[row_of[(bank, q)]][1]
@@ -335,8 +425,15 @@ def tile_minibatchdiscriminator_kernel(tc, tensor, T, out_0, out_1):
                         nc.tensor.matmul(out=s2[:, n:n + 1], lhsT=ets[bank][:, q, :], rhs=onesz[:], start=False, stop=(last_fin[2] == index))
                         nc.tensor.matmul(out=s1[par][:, n + 1 + par:n + 1 + par + P], lhsT=ets[bank][:, q, :], rhs=ident[:], is_transpose=True,
                                          start=False, stop=(last_fin[par] == index))
+                        if last_fin[par] == index:
+                            nc.vector.tensor_copy(out=s1c[par][:], in_=s1[par][:, 0:NX + 2])
+                        if last_fin[2] == index:
+                            nc.scalar.copy(out=s2c[:], in_=s2[:])
                     elif what == "warm":
-                        nc.tensor.matmul_mx(out=idle[:], lhsT=xq[:, 0:P].bitcast(FP8X4), lhsT_scale=xsc[:, 0:P],
+                        if len(idles) == 0:
+                            idle = psum.tile([P, 512], F32, name="idle", tag="b7")
+                            idles.append(idle)
+                        nc.tensor.matmul_mx(out=idles[0][:], lhsT=xq[:, 0:P].bitcast(FP8X4), lhsT_scale=xsc[:, 0:P],
                                             rhs=tq0[:, 0:512].bitcast(FP8X4), rhs_scale=tsc0[:, 0:512], start=True, stop=True)
                     elif what == "stt":
                         g, k, r = item[1], item[2], item[3]
@@ -374,45 +471,40 @@ def tile_minibatchdiscriminator_kernel(tc, tensor, T, out_0, out_1):
                             nc.vector.tensor_copy(out=fsx[:, 2 * i:2 * i + 2, N:NX], in_=fsx[:, 2 * i:2 * i + 2, 0:P])
                         else:
                             nc.vector.tensor_copy(out=snegx[:, N:NX], in_=snegx[:, 0:P])
+                    elif what == "sneg":
+                        nc.vector.tensor_scalar(out=snegx[:, 0:N], in0=sp[:], scalar1=-0.5, scalar2=None, op0=ALU.mult)
+                    elif what == "ssum":
+                        nc.scalar.copy(out=ssum[:], in_=sp[:])
                     else:
                         assert what == "xout"
-                        t, i = item[1], item[2]
-                        width = IN_F // XP
-                        if i == 0:
-                            xf = xop.tile([P, IN_F], F32, name="xf", tag="xf")
-                            x8 = xop.tile([P, IN_F], FP8, name="x8", tag="x8")
-                            xfs[t] = xf
-                            x8s[t] = x8
-                        if i < XP:
-                            cols = slice(i * width, (i + 1) * width)
-                            nc.vector.tensor_copy(out=xfs[t][:, cols], in_=xs[t][:, cols])
-                            if i == XP - 1:
-                                nc.sync.dma_start(out=out_0[t * P:(t + 1) * P, 0:IN_F], in_=xfs[t][:])
-                        else:
-                            cols = slice((i - XP) * width, (i - XP + 1) * width)
-                            nc.vector.tensor_scalar(out=x8s[t][:, cols], in0=xfs[t][:, cols], scalar1=Y_SCALE, scalar2=None, op0=ALU.mult,
-                                                    saturate=False)
-                            if i == 2 * XP - 1:
-                                nc.sync.dma_start(out=out_1[t * P:(t + 1) * P, 0:IN_F], in_=x8s[t][:].bitcast(U8))
+                        xout(item[1], item[2])
 
-            s1c = [xop.tile([P, NX + 2], F32, name="s1c%d" % i, tag="s1c%d" % i) for i in range(2)]
-            s2c = xop.tile([P, N], F32, name="s2c", tag="s2c")
-            nc.vector.tensor_copy(out=s1c[0][:], in_=s1[0][:])
-            nc.scalar.copy(out=s1c[1][:], in_=s1[1][:])
-            nc.vector.tensor_copy(out=s2c[:], in_=s2[:])
-
-            o0 = xop.tile([P, 2, J], F32, name="o0", tag="o0")
-            o8 = xop.tile([P, 2, J], FP8, name="o8", tag="o8")
-            pt = psum.tile([P, 2, J], F32, name="pt", tag="b0")
-            for t in range(2):
-                parts = [rowsum[:, t * P:(t + 1) * P], colx[:, t * P:(t + 1) * P], s2c[:, t * P:(t + 1) * P],
-                         s1c[0][:, t * P:(t + 1) * P], s1c[1][:, t * P + 1:(t + 1) * P + 1]]
-                if t == 0:
-                    parts = parts + [colx[:, N:NX], s1c[0][:, N:NX], s1c[1][:, N + 1:NX + 1]]
-                for i in range(len(parts)):
-                    nc.tensor.matmul(out=pt[:, t, :], lhsT=parts[i], rhs=ident[:], is_transpose=True, start=(i == 0), stop=(i == len(parts) - 1))
-            nc.vector.tensor_scalar(out=o0[:], in0=pt[:], scalar1=1.0, scalar2=None, op0=ALU.add)
-            nc.scalar.activation(out=o8[:], in_=o0[:], func=ACT.Copy, scale=Y_SCALE, saturate=False)
-            nc.sync.dma_start(out=out_0.rearrange("(t p) c -> p t c", p=P)[:, :, IN_F:IN_F + J], in_=o0[:])
-            for t in range(2):
-                nc.sync.dma_start(out=out_1[t * P:(t + 1) * P, IN_F:IN_F + J], in_=o8[:, t, :].bitcast(U8))
+                late = (rows[row_of[(prog[last_fin[2]][1], prog[last_fin[2]][2])]][1] + 1) % 2
+                pts = [psum.tile([P, J], F32, name="pt", tag="b%d" % t) for t in range(2)]
+                parts = [[], []]
+                for t in range(2):
+                    parts[t] = [rowsum[:, t * P:(t + 1) * P], colx[:, t * P:(t + 1) * P]]
+                parts[0].append(colx[:, N:NX])
+                early_count = [len(parts[0]), len(parts[1])]
+                for par in (1 - late, late):
+                    for t in range(2):
+                        parts[t].append(s1c[par][:, t * P + par:(t + 1) * P + par])
+                    parts[0].append(s1c[par][:, N + par:NX + par])
+                for t in range(2):
+                    parts[t].append(s2c[:, t * P:(t + 1) * P])
+                for t in range(2):
+                    for i in range(early_count[t]):
+                        nc.tensor.matmul(out=pts[t][:], lhsT=parts[t][i], rhs=ident[:], is_transpose=True, start=(i == 0), stop=False)
+                o0 = endp.tile([P, 2, J], F32, name="o0")
+                o8 = [endp.tile([P, J], FP8, name="o8%d" % t) for t in range(2)]
+                for t in range(2):
+                    for i in range(early_count[t], len(parts[t])):
+                        nc.tensor.matmul(out=pts[t][:], lhsT=parts[t][i], rhs=ident[:], is_transpose=True, start=False, stop=(i == len(parts[t]) - 1))
+                    if t == 0:
+                        nc.vector.tensor_copy(out=o0[:, t, :], in_=pts[t][:])
+                        nc.vector.tensor_scalar(out=o8[t][:], in0=pts[t][:], scalar1=Y_SCALE, scalar2=None, op0=ALU.mult, saturate=False)
+                    else:
+                        nc.scalar.copy(out=o0[:, t, :], in_=pts[t][:])
+                        nc.scalar.activation(out=o8[t][:], in_=pts[t][:], func=ACT.Copy, scale=Y_SCALE, saturate=False)
+                    nc.sync.dma_start(out=out_0[t * P:(t + 1) * P, IN_F:IN_F + J], in_=o0[:, t, :])
+                    nc.sync.dma_start(out=out_1[t * P:(t + 1) * P, IN_F:IN_F + J], in_=o8[t][:].bitcast(U8))

@@ -25,14 +25,15 @@ RV = 8
 RB = 4
 SINGLE = 0
 CV = 512
+XAT = 1
 NX = N + P
 XP = 4
 LEAD = 2
 XH1 = 8
 XH2 = 3
-NDUMMY = 14
-NDUMMY2 = 1
+XC1 = 2
 IDLE_HEAD = 3
+AHEAD = 5
 A_EARLY = 0
 B_EARLY = 0
 TB = 14
@@ -41,6 +42,7 @@ FIN_LAG = 2
 WARM_EVERY = 864
 WARM_FIRST = 64
 WARM_N = 3
+HOLD = 4
 LAG = 1
 B_STT = 0
 FIN_GAP = 12
@@ -212,7 +214,13 @@ def tile_minibatchdiscriminator_kernel(tc, tensor, T, out_0, out_1):
         xfs = {}
         x8s = {}
 
-        def xout(t, i):
+        def xstore(t, which):
+            if which == 0:
+                nc.sync.dma_start(out=out_0[t * P:(t + 1) * P, 0:IN_F], in_=xfs[t][:])
+            else:
+                nc.sync.dma_start(out=out_1[t * P:(t + 1) * P, 0:IN_F], in_=x8s[t][:].bitcast(U8))
+
+        def xout(t, i, store):
             width = IN_F // XP
             if i == 0:
                 xf = xop.tile([P, IN_F], F32, name="xf", tag="xf")
@@ -222,14 +230,14 @@ def tile_minibatchdiscriminator_kernel(tc, tensor, T, out_0, out_1):
             if i < XP:
                 cols = slice(i * width, (i + 1) * width)
                 nc.vector.tensor_copy(out=xfs[t][:, cols], in_=xs[t][:, cols])
-                if i == XP - 1:
-                    nc.sync.dma_start(out=out_0[t * P:(t + 1) * P, 0:IN_F], in_=xfs[t][:])
+                if i == XP - 1 and store:
+                    xstore(t, 0)
             else:
                 cols = slice((i - XP) * width, (i - XP + 1) * width)
                 nc.vector.tensor_scalar(out=x8s[t][:, cols], in0=xfs[t][:, cols], scalar1=Y_SCALE, scalar2=None, op0=ALU.mult,
                                         saturate=False)
-                if i == 2 * XP - 1:
-                    nc.sync.dma_start(out=out_1[t * P:(t + 1) * P, 0:IN_F], in_=x8s[t][:].bitcast(U8))
+                if i == 2 * XP - 1 and store:
+                    xstore(t, 1)
 
         with ExitStack() as pre:
             rawp = pre.enter_context(tc.tile_pool(name="rawp", bufs=8))
@@ -248,7 +256,7 @@ def tile_minibatchdiscriminator_kernel(tc, tensor, T, out_0, out_1):
                 raw = rawp.tile([P, 4, width], BF16, name="raw", tag="raw")
                 nc.sync.dma_start(out=raw[:], in_=tv[s][:, :, h * 1024 + c0:h * 1024 + c0 + width])
                 raws.append(raw)
-                if index == 1:
+                if index == XAT:
                     for t in range(2):
                         nc.sync.dma_start(out=xs[t][:], in_=tensor[t * P:(t + 1) * P, :])
 
@@ -266,8 +274,10 @@ def tile_minibatchdiscriminator_kernel(tc, tensor, T, out_0, out_1):
 
             def quantise(index):
                 s, h, c0, width = pieces[index]
-                nc.vector.quantize_mx(out=tqs[2 * s + h][:, c0:c0 + width].bitcast(FP8X4), scales=tscs[2 * s + h][:, c0:c0 + width],
-                                      in_=grps[index][:].rearrange("p c t -> p (c t)"))
+                for half in range(2):
+                    a, b = half * width // 2, (half + 1) * width // 2
+                    nc.vector.quantize_mx(out=tqs[2 * s + h][:, c0 + a:c0 + b].bitcast(FP8X4), scales=tscs[2 * s + h][:, c0 + a:c0 + b],
+                                          in_=grps[index][:, a:b, :].rearrange("p c t -> p (c t)"))
 
             fts = []
 
@@ -286,59 +296,76 @@ def tile_minibatchdiscriminator_kernel(tc, tensor, T, out_0, out_1):
                         )
 
             with tc.manual_schedule(engines=pinned):
-                wu = psum.tile([P, P], F32, name="wu", tag="b7")
-                for d in range(NDUMMY):
-                    nc.tensor.matmul(out=wu[:], lhsT=ident[:], rhs=ident[:], start=True, stop=True)
-                interleave(0)
-                interleave(1)
-                quantise(0)
-                quantise(1)
-                for piece in range(XH1):
-                    xout(piece // (2 * XP), piece % (2 * XP))
-                for g in range(PASSES):
-                    xt = psum.tile([P, 2, N], F32, name="xt", tag="b%d" % g)
-                    for t in range(2):
-                        words = xs[t][:].bitcast(F32)
-                        for u in range(2):
-                            nc.tensor.transpose(xt[:, u, t * P:(t + 1) * P], words[:, 256 * g + u:256 * (g + 1):2], ident[:])
-                    if g < NDUMMY2:
-                        nc.tensor.matmul(out=wu[:], lhsT=ident[:], rhs=ident[:], start=True, stop=True)
-                    nc.scalar.copy(out=xg[:, g, :, :].bitcast(F32), in_=xt[:].rearrange("p u n -> p n u"))
-                interleave(2)
-                nc.vector.quantize_mx(out=xq[:].bitcast(FP8X4), scales=xsc[:], in_=xg[:].rearrange("p g n f -> p (g n f)"))
-                for b in range(8):
-                    ft = psum.tile([P, 512], F32, name="ft", tag="b%d" % b)
-                    fts.append(ft)
-                multiply(0)
-                multiply(1)
-                for index in range(2, len(pieces)):
-                    if index + 1 < len(pieces):
-                        interleave(index + 1)
-                    quantise(index)
-                    multiply(index)
-                for w in range(4):
-                    for t in range(2):
-                        dst = fnat[t][:, :, 32 * w:32 * (w + 1)]
-                        view = fts[4 * t + w][:].rearrange("p (j k) -> p k j", k=K)
-                        if t == 0 and w != 0:
-                            nc.vector.tensor_copy(out=dst, in_=view)
-                        else:
-                            nc.scalar.copy(out=dst, in_=view)
+                ready = []
+                xts = []
+
+                def xcopy(g):
+                    nc.scalar.copy(out=xg[:, g, :, :].bitcast(F32), in_=xts[g][:].rearrange("p u n -> p n u"))
+
+                for index in range(len(pieces) + 1):
+                    if index == XAT + 1:
+                        for g in range(PASSES):
+                            xt = psum.tile([P, 2, N], F32, name="xt", tag="b%d" % g)
+                            xts.append(xt)
+                            for t in range(2):
+                                words = xs[t][:].bitcast(F32)
+                                for u in range(2):
+                                    nc.tensor.transpose(xt[:, u, t * P:(t + 1) * P], words[:, 256 * g + u:256 * (g + 1):2], ident[:])
+                        for piece in range(XH1):
+                            xout(piece // (2 * XP), piece % (2 * XP), False)
+                        for g in range(XC1):
+                            xcopy(g)
+                        quantise(index - 1)
+                    if index < len(pieces):
+                        interleave(index)
+                    if index == XAT + 1:
+                        for g in range(XC1, PASSES):
+                            xcopy(g)
+                    if index >= 1:
+                        if index != XAT + 1:
+                            quantise(index - 1)
+                        ready.append(index - 1)
+                    if index == XAT + 2:
+                        nc.vector.quantize_mx(out=xq[:].bitcast(FP8X4), scales=xsc[:], in_=xg[:].rearrange("p g n f -> p (g n f)"))
+                        for b in range(8):
+                            ft = psum.tile([P, 512], F32, name="ft", tag="b%d" % b)
+                            fts.append(ft)
+                    if index >= XAT + 2:
+                        for done in ready:
+                            multiply(done)
+                        ready = []
+                for t, w, engine in ((0, 0, "s"), (0, 1, "s"), (0, 2, "v"), (0, 3, "v"), (1, 0, "s"), (1, 1, "s"), (1, 3, "v"), (1, 2, "s")):
+                    dst = fnat[t][:, :, 32 * w:32 * (w + 1)]
+                    view = fts[4 * t + w][:].rearrange("p (j k) -> p k j", k=K)
+                    if engine == "v":
+                        nc.vector.tensor_copy(out=dst, in_=view)
+                    else:
+                        nc.scalar.copy(out=dst, in_=view)
                 idleh = psum.tile([P, 512], F32, name="idleh", tag="b0")
                 for i in range(IDLE_HEAD):
                     nc.tensor.matmul_mx(out=idleh[:], lhsT=xq[:, 0:P].bitcast(FP8X4), lhsT_scale=xsc[:, 0:P],
                                         rhs=tq0[:, 0:512].bitcast(FP8X4), rhs_scale=tsc0[:, 0:512], start=True, stop=True)
                 for piece in range(XH1, XH1 + XH2):
-                    xout(piece // (2 * XP), piece % (2 * XP))
-                for b in range(8):
-                    fpb = psum.tile([P, 2, N], F32, name="fp", tag="b%d" % (b % 7))
+                    xout(piece // (2 * XP), piece % (2 * XP), False)
+                fpbs = []
+
+                def turn(b, t):
+                    if t == 0:
+                        fpb = psum.tile([P, 2, N], F32, name="fp", tag="b%d" % (b % 7))
+                        fpbs.append(fpb)
                     for kk in range(2):
-                        for t in range(2):
-                            nc.tensor.transpose(fpb[:, kk, t * P:(t + 1) * P], fnat[t][:, 2 * b + kk, :], ident[:])
+                        nc.tensor.transpose(fpbs[b][:, kk, t * P:(t + 1) * P], fnat[t][:, 2 * b + kk, :], ident[:])
+
+                for b in range(AHEAD):
+                    turn(b, 0)
+                for b in range(8):
+                    turn(b, 1)
                     if b % 2 == 0:
-                        nc.scalar.copy(out=fsx[:, 2 * b:2 * b + 2, 0:N], in_=fpb[:])
+                        nc.scalar.copy(out=fsx[:, 2 * b:2 * b + 2, 0:N], in_=fpbs[b][:])
                     else:
-                        nc.vector.tensor_copy(out=fsx[:, 2 * b:2 * b + 2, 0:N], in_=fpb[:])
+                        nc.vector.tensor_copy(out=fsx[:, 2 * b:2 * b + 2, 0:N], in_=fpbs[b][:])
+                    if b + AHEAD < 8:
+                        turn(b + AHEAD, 0)
                 sp = psum.tile([P, N], F32, name="sp", tag="b7")
                 for k in range(K):
                     for t in range(2):
@@ -381,6 +408,14 @@ def tile_minibatchdiscriminator_kernel(tc, tensor, T, out_0, out_1):
                 for acc0, width in ((s1[0], 512), (s1[1], 512), (s2, N)):
                     for c in range(width // P):
                         nc.tensor.matmul(out=acc0[:, c * P:(c + 1) * P], lhsT=zero[:], rhs=ident[:], is_transpose=True, start=(c == 0), stop=False)
+
+                for piece in range(XH1 + XH2):
+                    if piece % XP == XP - 1:
+                        xstore(piece // (2 * XP), (piece % (2 * XP)) // XP)
+                hold = psum.tile([P, 512], F32, name="hold", tag="b3")
+                for i in range(HOLD):
+                    nc.tensor.matmul_mx(out=hold[:], lhsT=xq[:, 0:P].bitcast(FP8X4), lhsT_scale=xsc[:, 0:P],
+                                        rhs=tq0[:, 0:512].bitcast(FP8X4), rhs_scale=tsc0[:, 0:512], start=True, stop=True)
 
                 for index in range(len(prog)):
                     item = prog[index]
@@ -477,7 +512,7 @@ def tile_minibatchdiscriminator_kernel(tc, tensor, T, out_0, out_1):
                         nc.scalar.copy(out=ssum[:], in_=sp[:])
                     else:
                         assert what == "xout"
-                        xout(item[1], item[2])
+                        xout(item[1], item[2], True)
 
                 late = (rows[row_of[(prog[last_fin[2]][1], prog[last_fin[2]][2])]][1] + 1) % 2
                 pts = [psum.tile([P, J], F32, name="pt", tag="b%d" % t) for t in range(2)]

@@ -29,6 +29,8 @@ XAT = 1
 NX = N + P
 XP = 4
 LEAD = 2
+B_LEAD = 12
+SIDE_FIRST = 40
 XH1 = 8
 XH2 = 3
 XC1 = 2
@@ -42,9 +44,9 @@ FIN_LAG = 2
 WARM_EVERY = 864
 WARM_FIRST = 64
 WARM_N = 3
-HOLD = 4
+HOLD = 0
 LAG = 1
-B_STT = 0
+B_STT = 40
 FIN_GAP = 12
 
 
@@ -65,7 +67,7 @@ def build_program():
     exp_due = {}
     fin_due = {}
     groups = []
-    side = [("xout", t, i) for t in range(2) for i in range(2 * XP)][XH1 + XH2:] + [("wrap", i) for i in range(K // 2)] + [("sneg",), ("wrap", K // 2)]
+    side = [("xout", t, i) for t in range(2) for i in range(2 * XP)][XH1 + XH2:] + [("wrap", i) for i in range(K // 2 + 1)]
 
     def new_row(kind):
         if open_bank[kind] is None or open_bank[kind][1] == banks[open_bank[kind][0]][1]:
@@ -124,10 +126,10 @@ def build_program():
         vector = []
         scalar = []
         if step < LEAD:
-            first = step * len(side) // LEAD
-            vector = side[first:(step + 1) * len(side) // LEAD]
             if step == LEAD - 1:
+                vector.append(("sneg",))
                 scalar.append(("ssum",))
+            vector = vector + make("B", B_LEAD)
         cs = step - LEAD
         if 0 <= cs < c_steps:
             g, k = divmod(cs, K)
@@ -139,7 +141,9 @@ def build_program():
                 alone.append(("cadd", g - 1, k - 1))
             if g >= 1 and k == RV + 2:
                 alone.append(("cadd", g - 1, 0))
-            vector = weave(alone, make("B", share(NB * K, cs, b_steps)) if cs < b_steps else [])
+            if SIDE_FIRST <= cs < SIDE_FIRST + len(side):
+                alone.append(side[cs - SIDE_FIRST])
+            vector = weave(alone, make("B", share(NB * K - LEAD * B_LEAD, cs, b_steps)) if cs < b_steps else [])
             if g >= 1 and k < RV:
                 scalar.append(("cexp", g - 1, k))
         if cs == c_steps:
@@ -165,9 +169,9 @@ def build_program():
             st, rid, k = made[state["taken"]]
             state["taken"] += 1
             kind, n, bank, q, opened = rows[rid]
-            if opened and k == 0:
-                pe(("tp", rid, -1))
             pe(("tp", rid, k))
+            if opened and k == K - 1:
+                pe(("tp", rid, K))
             if k == K - 1 and q == banks[bank][1] - 1:
                 exp_due.setdefault(step + LAG, []).append(bank)
                 state["open"] += 1
@@ -429,10 +433,10 @@ def tile_minibatchdiscriminator_kernel(tc, tensor, T, out_0, out_1):
                         if what == "abs":
                             nc.scalar.activation(out=terms[rid][:, k, :], in_=fsx[:, k, n + 1:n + 1 + P], func=ACT.Abs, scale=-1.0,
                                                  bias=fsx[:, k, n:n + 1])
-                        elif k == 0 and not rows[rid][4]:
+                        elif k == K - 1 and not rows[rid][4]:
                             nc.vector.scalar_tensor_tensor(out=terms[rid][:, k, :], in0=fsx[:, k, n + 1:n + 1 + P], scalar=fsx[:, k, n:n + 1],
                                                            in1=snegx[:, n + 1:n + 1 + P], op0=ALU.max, op1=ALU.add)
-                        elif k == (0 if rows[rid][4] else 1):
+                        elif k == K - 2:
                             nc.vector.tensor_scalar(out=terms[rid][:, k, :], in0=fsx[:, k, n + 1:n + 1 + P], scalar1=fsx[:, k, n:n + 1],
                                                     scalar2=snegx[:, n:n + 1], op0=ALU.max, op1=ALU.add)
                         else:
@@ -441,12 +445,12 @@ def tile_minibatchdiscriminator_kernel(tc, tensor, T, out_0, out_1):
                     elif what == "tp":
                         rid, k = item[1], item[2]
                         kind, n, bank, q, opened = rows[rid]
-                        first = (k == -1) if opened else (k == 0)
+                        first = (k == 0)
                         if first and q == 0:
                             lt = psum.tile([P, RB, P], F32, name="lt", tag=bank_tag[bank])
                             lts[bank] = lt
-                        nc.tensor.matmul(out=lts[bank][:, q, :], lhsT=(snegx[:, n + 1:n + 1 + P] if k == -1 else terms[rid][:, k, :]), rhs=ident[:],
-                                         is_transpose=True, start=first, stop=(k == K - 1))
+                        nc.tensor.matmul(out=lts[bank][:, q, :], lhsT=(snegx[:, n + 1:n + 1 + P] if k == K else terms[rid][:, k, :]), rhs=ident[:],
+                                         is_transpose=True, start=first, stop=(k == (K if opened else K - 1)))
                     elif what == "bexp":
                         bank = item[1]
                         kind, size = banks[bank]

@@ -47,6 +47,7 @@ WARM_N = 3
 HOLD = 0
 LAG = 1
 B_STT = 40
+ROWN = 32
 FIN_GAP = 12
 
 
@@ -201,7 +202,7 @@ def tile_minibatchdiscriminator_kernel(tc, tensor, T, out_0, out_1):
         ssum = cst.tile([P, N], F32, name="ssum")
         fsx = cst.tile([P, K, NX], F32, name="fsx")
         zero = cst.tile([P, P], F32, name="zero")
-        onesz = cst.tile([P, 1], F32, name="onesz")
+        onesz = cst.tile([P, ROWN], F32, name="onesz")
         xs = [cst.tile([P, IN_F], BF16, name="xs%d" % t) for t in range(2)]
         xq = cst.tile([P, PASSES * N], U32, name="xq", align_bytes=64)
         xsc = cst.tile([P, PASSES * N], U8, name="xsc", align_bytes=64)
@@ -213,7 +214,8 @@ def tile_minibatchdiscriminator_kernel(tc, tensor, T, out_0, out_1):
         nc.gpsimd.memset(colx[:, 0:N], 1.0)
         nc.gpsimd.memset(colx[:, N:NX], 0.0)
         nc.gpsimd.memset(zero[:], 0.0)
-        nc.vector.tensor_scalar(out=onesz[:], in0=ident[:, P - 1:P], scalar1=-1.0, scalar2=1.0, op0=ALU.mult, op1=ALU.add)
+        nc.gpsimd.memset(onesz[:], 0.0)
+        nc.vector.tensor_scalar(out=onesz[:, 0:1], in0=ident[:, P - 1:P], scalar1=-1.0, scalar2=1.0, op0=ALU.mult, op1=ALU.add)
 
         xfs = {}
         x8s = {}
@@ -408,8 +410,8 @@ def tile_minibatchdiscriminator_kernel(tc, tensor, T, out_0, out_1):
             idles = []
             with tc.manual_schedule(engines=pinned):
                 s1 = [psum.tile([P, 512], F32, name="s1", tag="b%d" % (4 + i)) for i in range(2)]
-                s2 = psum.tile([P, N], F32, name="s2", tag="b6")
-                for acc0, width in ((s1[0], 512), (s1[1], 512), (s2, N)):
+                s2 = psum.tile([P, 512], F32, name="s2", tag="b6")
+                for acc0, width in ((s1[0], 512), (s1[1], 512), (s2, 512)):
                     for c in range(width // P):
                         nc.tensor.matmul(out=acc0[:, c * P:(c + 1) * P], lhsT=zero[:], rhs=ident[:], is_transpose=True, start=(c == 0), stop=False)
 
@@ -461,13 +463,13 @@ def tile_minibatchdiscriminator_kernel(tc, tensor, T, out_0, out_1):
                         bank, q = item[1], item[2]
                         n = rows[row_of[(bank, q)]][1]
                         par = (n + 1) % 2
-                        nc.tensor.matmul(out=s2[:, n:n + 1], lhsT=ets[bank][:, q, :], rhs=onesz[:], start=False, stop=(last_fin[2] == index))
+                        nc.tensor.matmul(out=s2[:, n:n + ROWN], lhsT=ets[bank][:, q, :], rhs=onesz[:], start=False, stop=(last_fin[2] == index))
                         nc.tensor.matmul(out=s1[par][:, n + 1 + par:n + 1 + par + P], lhsT=ets[bank][:, q, :], rhs=ident[:], is_transpose=True,
                                          start=False, stop=(last_fin[par] == index))
                         if last_fin[par] == index:
                             nc.vector.tensor_copy(out=s1c[par][:], in_=s1[par][:, 0:NX + 2])
                         if last_fin[2] == index:
-                            nc.scalar.copy(out=s2c[:], in_=s2[:])
+                            nc.scalar.copy(out=s2c[:], in_=s2[:, 0:N])
                     elif what == "warm":
                         if len(idles) == 0:
                             idle = psum.tile([P, 512], F32, name="idle", tag="b7")

@@ -29,7 +29,7 @@ XAT = 1
 NX = N + P
 XP = 4
 LEAD = 2
-B_LEAD = 12
+B_LEAD = (14,22)
 SIDE_FIRST = 40
 XH1 = 8
 XH2 = 3
@@ -41,10 +41,10 @@ B_EARLY = 0
 TB = 14
 EB = 8
 FIN_LAG = 2
-WARM_EVERY = 864
-WARM_FIRST = 64
+WARM_EVERY = 1000
+WARM_FIRST = 800
 WARM_N = 3
-HOLD = 0
+HOLD = 3
 LAG = 1
 B_STT = 40
 ROWN = 32
@@ -130,7 +130,7 @@ def build_program():
             if step == LEAD - 1:
                 vector.append(("sneg",))
                 scalar.append(("ssum",))
-            vector = vector + make("B", B_LEAD)
+            vector = vector + make("B", B_LEAD[step])
         cs = step - LEAD
         if 0 <= cs < c_steps:
             g, k = divmod(cs, K)
@@ -144,7 +144,7 @@ def build_program():
                 alone.append(("cadd", g - 1, 0))
             if SIDE_FIRST <= cs < SIDE_FIRST + len(side):
                 alone.append(side[cs - SIDE_FIRST])
-            vector = weave(alone, make("B", share(NB * K - LEAD * B_LEAD, cs, b_steps)) if cs < b_steps else [])
+            vector = weave(alone, make("B", share(NB * K - sum(B_LEAD), cs, b_steps)) if cs < b_steps else [])
             if g >= 1 and k < RV:
                 scalar.append(("cexp", g - 1, k))
         if cs == c_steps:

@@ -33,6 +33,7 @@ B_LEAD = (14,22)
 SIDE_FIRST = 40
 XH1 = 8
 XH2 = 3
+XL = 3
 XC1 = 2
 IDLE_HEAD = 3
 AHEAD = 5
@@ -46,7 +47,7 @@ WARM_FIRST = 800
 WARM_N = 3
 HOLD = 3
 LAG = 1
-B_STT = 40
+B_STT = 0
 ROWN = 32
 FIN_GAP = 12
 
@@ -68,7 +69,7 @@ def build_program():
     exp_due = {}
     fin_due = {}
     groups = []
-    side = [("xout", t, i) for t in range(2) for i in range(2 * XP)][XH1 + XH2:] + [("wrap", i) for i in range(K // 2 + 1)]
+    side = [("xout", t, i) for t in range(2) for i in range(2 * XP)][XH1 + XH2 + XL:] + [("wrap", i) for i in range(K // 2 + 1)]
 
     def new_row(kind):
         if open_bank[kind] is None or open_bank[kind][1] == banks[open_bank[kind][0]][1]:
@@ -131,6 +132,8 @@ def build_program():
                 vector.append(("sneg",))
                 scalar.append(("ssum",))
             vector = vector + make("B", B_LEAD[step])
+            if step == 0:
+                vector = vector + [("xout", t, i) for t in range(2) for i in range(2 * XP)][XH1 + XH2:XH1 + XH2 + XL]
         cs = step - LEAD
         if 0 <= cs < c_steps:
             g, k = divmod(cs, K)

@@ -42,8 +42,8 @@ B_EARLY = 0
 TB = 14
 EB = 8
 FIN_LAG = 2
-WARM_EVERY = 1000
-WARM_FIRST = 800
+WARM_EVERY = 4000
+WARM_FIRST = 1700
 WARM_N = 3
 HOLD = 3
 LAG = 1

@@ -18,12 +18,11 @@ ACT = mybir.ActivationFunctionType
 
 P = 128
 PASSES = 4
-NA = 104
-NB = 80
+NA = 102
+NB = 82
 NC = 72
 RV = 8
 RB = 4
-SINGLE = 0
 CV = 512
 XAT = 1
 NX = N + P
@@ -47,7 +46,7 @@ WARM_FIRST = 1700
 WARM_N = 3
 HOLD = 3
 LAG = 1
-B_STT = 0
+B_STT = 24
 ROWN = 32
 FIN_GAP = 12
 
@@ -73,7 +72,7 @@ def build_program():
 
     def new_row(kind):
         if open_bank[kind] is None or open_bank[kind][1] == banks[open_bank[kind][0]][1]:
-            banks.append((kind, RB if left[kind] > SINGLE else 1))
+            banks.append((kind, min(RB, left[kind])))
             open_bank[kind] = [len(banks) - 1, 0]
         bank, q = open_bank[kind]
         open_bank[kind][1] += 1

from contextlib import ExitStack

import concourse.mybir as mybir
from concourse.masks import make_identity

N, IN_F, J, K = 256, 2048, 128, 16
Y_SCALE = 110.0
FLOPS = 2 * N * IN_F * J * K + 3 * N * N * J * K

F32 = mybir.dt.float32
BF16 = mybir.dt.bfloat16
U32 = mybir.dt.uint32
U8 = mybir.dt.uint8
FP8X4 = mybir.dt.float8_e4m3fn_x4
FP8 = mybir.dt.float8_e4m3fn
ALU = mybir.AluOpType
ACT = mybir.ActivationFunctionType

P = 128
PASSES = 4
NA = 102
NB = 82
NC = 72
RV = 8
RB = 4
CV = 512
XAT = 1
NX = N + P
XP = 4
LEAD = 2
B_LEAD = (14,22)
SIDE_FIRST = 40
XH1 = 8
XH2 = 3
XL = 3
XC1 = 2
IDLE_HEAD = 3
AHEAD = 5
A_EARLY = 0
B_EARLY = 0
TB = 14
EB = 8
FIN_LAG = 2
WARM_EVERY = 4000
WARM_FIRST = 1700
WARM_N = 3
HOLD = 3
LAG = 1
B_STT = 24
ROWN = 32
FIN_GAP = 12


def build_program():
    prog = []
    c_steps = (NC // RV) * K
    steps = LEAD + c_steps
    a_steps = steps - A_EARLY
    b_steps = c_steps - B_EARLY
    rows = []
    banks = []
    open_bank = {"A": None, "B": None}
    made = []
    state = {"row": 0, "pe": 0, "taken": 0, "fins": 0, "gap": 0, "open": 0}
    fins = []
    cur = {"A": None, "B": None}
    left = {"A": NA, "B": NB}
    exp_due = {}
    fin_due = {}
    groups = []
    side = [("xout", t, i) for t in range(2) for i in range(2 * XP)][XH1 + XH2 + XL:] + [("wrap", i) for i in range(K // 2 + 1)]

    def new_row(kind):
        if open_bank[kind] is None or open_bank[kind][1] == banks[open_bank[kind][0]][1]:
            banks.append((kind, min(RB, left[kind])))
            open_bank[kind] = [len(banks) - 1, 0]
        bank, q = open_bank[kind]
        open_bank[kind][1] += 1
        done = NB - left["B"]
        rows.append((kind, state["row"], bank, q, kind == "B" and (done + 1) * B_STT // NB == done * B_STT // NB))
        state["row"] += 1
        left[kind] -= 1
        return len(rows) - 1

    def make(kind, count):
        items = []
        for i in range(count):
            if cur[kind] is None:
                cur[kind] = [new_row(kind), 0]
            rid, k = cur[kind]
            items.append(("abs" if kind == "A" else "ts", rid, k))
            cur[kind][1] += 1
            if cur[kind][1] == K:
                cur[kind] = None
        return items

    def weave(first, second):
        woven = []
        total = len(first) + len(second)
        taken = 0
        for i in range(total):
            if (taken + 1) * total <= (i + 1) * len(first):
                woven.append(first[taken])
                taken += 1
            else:
                woven.append(second[i - taken])
        return woven

    def pe(item):
        prog.append(item)
        state["pe"] += 1
        if state["pe"] % WARM_EVERY == WARM_FIRST:
            for i in range(WARM_N):
                prog.append(("warm",))

    def fin_one():
        pe(("fin", fins[state["fins"]][0], fins[state["fins"]][1]))
        state["fins"] += 1
        state["gap"] = 0

    def share(total, step, over):
        return (step + 1) * total // over - step * total // over

    ng = NC // RV
    step = 0
    while step < steps or state["taken"] < len(made) or state["open"] > 0 or state["fins"] < len(fins):
        vector = []
        scalar = []
        if step < LEAD:
            if step == LEAD - 1:
                vector.append(("sneg",))
                scalar.append(("ssum",))
            vector = vector + make("B", B_LEAD[step])
            if step == 0:
                vector = vector + [("xout", t, i) for t in range(2) for i in range(2 * XP)][XH1 + XH2:XH1 + XH2 + XL]
        cs = step - LEAD
        if 0 <= cs < c_steps:
            g, k = divmod(cs, K)
            if k == 0:
                groups.append(state["row"])
                state["row"] += RV
            alone = [("stt", g, k, r) for r in range(RV)]
            if g >= 1 and 2 <= k < RV + 2:
                alone.append(("cadd", g - 1, k - 1))
            if g >= 1 and k == RV + 2:
                alone.append(("cadd", g - 1, 0))
            if SIDE_FIRST <= cs < SIDE_FIRST + len(side):
                alone.append(side[cs - SIDE_FIRST])
            vector = weave(alone, make("B", share(NB * K - sum(B_LEAD), cs, b_steps)) if cs < b_steps else [])
            if g >= 1 and k < RV:
                scalar.append(("cexp", g - 1, k))
        if cs == c_steps:
            for r in range(RV):
                vector.append(("cexp", ng - 1, r))
                vector.append(("cadd", ng - 1, r + 1))
            vector.append(("cadd", ng - 1, 0))
        if step < a_steps:
            scalar = scalar + make("A", share(NA * K, step, a_steps))
        for item in vector + scalar:
            prog.append(item)
        for item in scalar + vector:
            if item[0] == "ts" or item[0] == "abs":
                made.append((step, item[1], item[2]))
        for bank in exp_due.get(step, []):
            prog.append(("bexp", bank))
            fin_due.setdefault(step + FIN_LAG, []).append(bank)
        for bank in fin_due.get(step, []):
            state["open"] -= 1
            for q in range(banks[bank][1]):
                fins.append((bank, q))
        while state["taken"] < len(made) and made[state["taken"]][0] + LAG <= step:
            st, rid, k = made[state["taken"]]
            state["taken"] += 1
            kind, n, bank, q, opened = rows[rid]
            pe(("tp", rid, k))
            if opened and k == K - 1:
                pe(("tp", rid, K))
            if k == K - 1 and q == banks[bank][1] - 1:
                exp_due.setdefault(step + LAG, []).append(bank)
                state["open"] += 1
            state["gap"] += 1
            if state["gap"] >= FIN_GAP and state["fins"] < len(fins):
                fin_one()
        if step >= steps - 1:
            while state["fins"] < len(fins):
                fin_one()
        step += 1
    assert state["row"] == N and state["taken"] == len(made) == (NA + NB) * K
    return prog, rows, banks, groups


def tile_minibatchdiscriminator_kernel(tc, tensor, T, out_0, out_1):
    nc = tc.nc
    pinned = {mybir.EngineType.DVE, mybir.EngineType.PE, mybir.EngineType.Activation}
    with ExitStack() as ctx:
        cst = ctx.enter_context(tc.tile_pool(name="cst", bufs=1))
        xop = ctx.enter_context(tc.tile_pool(name="xop", bufs=2))
        psum = ctx.enter_context(tc.psum_pool(name="psum", bufs=1))

        ident = cst.tile([P, P], F32, name="ident")
        rowsum = cst.tile([P, N], F32, name="rowsum")
        colx = cst.tile([P, NX], F32, name="colx")
        snegx = cst.tile([P, NX], F32, name="snegx")
        ssum = cst.tile([P, N], F32, name="ssum")
        fsx = cst.tile([P, K, NX], F32, name="fsx")
        zero = cst.tile([P, P], F32, name="zero")
        onesz = cst.tile([P, ROWN], F32, name="onesz")
        xs = [cst.tile([P, IN_F], BF16, name="xs%d" % t) for t in range(2)]
        xq = cst.tile([P, PASSES * N], U32, name="xq", align_bytes=64)
        xsc = cst.tile([P, PASSES * N], U8, name="xsc", align_bytes=64)
        tq0 = cst.tile([P, 1024], U32, name="tq0", align_bytes=64)
        tsc0 = cst.tile([P, 1024], U8, name="tsc0", align_bytes=64)

        make_identity(nc, ident[:])
        nc.gpsimd.memset(rowsum[:], 0.0)
        nc.gpsimd.memset(colx[:, 0:N], 1.0)
        nc.gpsimd.memset(colx[:, N:NX], 0.0)
        nc.gpsimd.memset(zero[:], 0.0)
        nc.gpsimd.memset(onesz[:], 0.0)
        nc.vector.tensor_scalar(out=onesz[:, 0:1], in0=ident[:, P - 1:P], scalar1=-1.0, scalar2=1.0, op0=ALU.mult, op1=ALU.add)

        xfs = {}
        x8s = {}

        def xstore(t, which):
            if which == 0:
                nc.sync.dma_start(out=out_0[t * P:(t + 1) * P, 0:IN_F], in_=xfs[t][:])
            else:
                nc.sync.dma_start(out=out_1[t * P:(t + 1) * P, 0:IN_F], in_=x8s[t][:].bitcast(U8))

        def xout(t, i, store):
            width = IN_F // XP
            if i == 0:
                xf = xop.tile([P, IN_F], F32, name="xf", tag="xf")
                x8 = xop.tile([P, IN_F], FP8, name="x8", tag="x8")
                xfs[t] = xf
                x8s[t] = x8
            if i < XP:
                cols = slice(i * width, (i + 1) * width)
                nc.vector.tensor_copy(out=xfs[t][:, cols], in_=xs[t][:, cols])
                if i == XP - 1 and store:
                    xstore(t, 0)
            else:
                cols = slice((i - XP) * width, (i - XP + 1) * width)
                nc.vector.tensor_scalar(out=x8s[t][:, cols], in0=xfs[t][:, cols], scalar1=Y_SCALE, scalar2=None, op0=ALU.mult,
                                        saturate=False)
                if i == 2 * XP - 1 and store:
                    xstore(t, 1)

        with ExitStack() as pre:
            rawp = pre.enter_context(tc.tile_pool(name="rawp", bufs=8))
            grpp = pre.enter_context(tc.tile_pool(name="grpp", bufs=3))
            keep = pre.enter_context(tc.tile_pool(name="keep", bufs=1))
            tqs = [tq0] + [keep.tile([P, 1024], U32, name="tq%d" % i, align_bytes=64) for i in range(1, 2 * PASSES)]
            tscs = [tsc0] + [keep.tile([P, 1024], U8, name="tsc%d" % i, align_bytes=64) for i in range(1, 2 * PASSES)]
            xg = keep.tile([P, PASSES, N, 4], BF16, name="xg", align_bytes=64)
            fnat = [keep.tile([P, K, J], F32, name="fnat%d" % t) for t in range(2)]

            tv = T.rearrange("(s p t) j k -> s p t (j k)", p=P, t=4)
            pieces = [(0, 0, 0, 512), (0, 0, 512, 512)] + [(s, h, 0, 1024) for s in range(PASSES) for h in range(2)][1:]
            raws = []
            for index in range(len(pieces)):
                s, h, c0, width = pieces[index]
                raw = rawp.tile([P, 4, width], BF16, name="raw", tag="raw")
                nc.sync.dma_start(out=raw[:], in_=tv[s][:, :, h * 1024 + c0:h * 1024 + c0 + width])
                raws.append(raw)
                if index == XAT:
                    for t in range(2):
                        nc.sync.dma_start(out=xs[t][:], in_=tensor[t * P:(t + 1) * P, :])

            grps = {}

            def interleave(index):
                s, h, c0, width = pieces[index]
                cv = width * CV // 1024
                grp = grpp.tile([P, width, 4], BF16, name="grp", tag="grp", align_bytes=64)
                grps[index] = grp
                nc.vector.tensor_copy(out=grp[:, 0:cv, :].rearrange("p (c i) t -> p c t i", i=4),
                                      in_=raws[index][:, :, 0:cv].rearrange("p t (c i) -> p c t i", i=4))
                nc.scalar.copy(out=grp[:, cv:width, :].rearrange("p (c i) t -> p c t i", i=4),
                               in_=raws[index][:, :, cv:width].rearrange("p t (c i) -> p c t i", i=4))

            def quantise(index):
                s, h, c0, width = pieces[index]
                for half in range(2):
                    a, b = half * width // 2, (half + 1) * width // 2
                    nc.vector.quantize_mx(out=tqs[2 * s + h][:, c0 + a:c0 + b].bitcast(FP8X4), scales=tscs[2 * s + h][:, c0 + a:c0 + b],
                                          in_=grps[index][:, a:b, :].rearrange("p c t -> p (c t)"))

            fts = []

            def multiply(index):
                s, h, c0, width = pieces[index]
                for w in range(c0 // 512, (c0 + width) // 512):
                    for t in range(2):
                        nc.tensor.matmul_mx(
                            out=fts[4 * t + 2 * h + w][:],
                            lhsT=xq[:, s * N + t * P:s * N + (t + 1) * P].bitcast(FP8X4),
                            lhsT_scale=xsc[:, s * N + t * P:s * N + (t + 1) * P],
                            rhs=tqs[2 * s + h][:, 512 * w:512 * (w + 1)].bitcast(FP8X4),
                            rhs_scale=tscs[2 * s + h][:, 512 * w:512 * (w + 1)],
                            start=(s == 0),
                            stop=(s == PASSES - 1),
                        )

            with tc.manual_schedule(engines=pinned):
                ready = []
                xts = []

                def xcopy(g):
                    nc.scalar.copy(out=xg[:, g, :, :].bitcast(F32), in_=xts[g][:].rearrange("p u n -> p n u"))

                for index in range(len(pieces) + 1):
                    if index == XAT + 1:
                        for g in range(PASSES):
                            xt = psum.tile([P, 2, N], F32, name="xt", tag="b%d" % g)
                            xts.append(xt)
                            for t in range(2):
                                words = xs[t][:].bitcast(F32)
                                for u in range(2):
                                    nc.tensor.transpose(xt[:, u, t * P:(t + 1) * P], words[:, 256 * g + u:256 * (g + 1):2], ident[:])
                        for piece in range(XH1):
                            xout(piece // (2 * XP), piece % (2 * XP), False)
                        for g in range(XC1):
                            xcopy(g)
                        quantise(index - 1)
                    if index < len(pieces):
                        interleave(index)
                    if index == XAT + 1:
                        for g in range(XC1, PASSES):
                            xcopy(g)
                    if index >= 1:
                        if index != XAT + 1:
                            quantise(index - 1)
                        ready.append(index - 1)
                    if index == XAT + 2:
                        nc.vector.quantize_mx(out=xq[:].bitcast(FP8X4), scales=xsc[:], in_=xg[:].rearrange("p g n f -> p (g n f)"))
                        for b in range(8):
                            ft = psum.tile([P, 512], F32, name="ft", tag="b%d" % b)
                            fts.append(ft)
                    if index >= XAT + 2:
                        for done in ready:
                            multiply(done)
                        ready = []
                for t, w, engine in ((0, 0, "s"), (0, 1, "s"), (0, 2, "v"), (0, 3, "v"), (1, 0, "s"), (1, 1, "s"), (1, 3, "v"), (1, 2, "s")):
                    dst = fnat[t][:, :, 32 * w:32 * (w + 1)]
                    view = fts[4 * t + w][:].rearrange("p (j k) -> p k j", k=K)
                    if engine == "v":
                        nc.vector.tensor_copy(out=dst, in_=view)
                    else:
                        nc.scalar.copy(out=dst, in_=view)
                idleh = psum.tile([P, 512], F32, name="idleh", tag="b0")
                for i in range(IDLE_HEAD):
                    nc.tensor.matmul_mx(out=idleh[:], lhsT=xq[:, 0:P].bitcast(FP8X4), lhsT_scale=xsc[:, 0:P],
                                        rhs=tq0[:, 0:512].bitcast(FP8X4), rhs_scale=tsc0[:, 0:512], start=True, stop=True)
                for piece in range(XH1, XH1 + XH2):
                    xout(piece // (2 * XP), piece % (2 * XP), False)
                fpbs = []

                def turn(b, t):
                    if t == 0:
                        fpb = psum.tile([P, 2, N], F32, name="fp", tag="b%d" % (b % 7))
                        fpbs.append(fpb)
                    for kk in range(2):
                        nc.tensor.transpose(fpbs[b][:, kk, t * P:(t + 1) * P], fnat[t][:, 2 * b + kk, :], ident[:])

                for b in range(AHEAD):
                    turn(b, 0)
                for b in range(8):
                    turn(b, 1)
                    if b % 2 == 0:
                        nc.scalar.copy(out=fsx[:, 2 * b:2 * b + 2, 0:N], in_=fpbs[b][:])
                    else:
                        nc.vector.tensor_copy(out=fsx[:, 2 * b:2 * b + 2, 0:N], in_=fpbs[b][:])
                    if b + AHEAD < 8:
                        turn(b + AHEAD, 0)
                sp = psum.tile([P, N], F32, name="sp", tag="b7")
                for k in range(K):
                    for t in range(2):
                        nc.tensor.matmul(out=sp[:, t * P:(t + 1) * P], lhsT=fnat[t][:, k, :], rhs=ident[:], is_transpose=True,
                                         start=(k == 0 and t == 0), stop=(k == K - 1 and t == 1))

        with ExitStack() as mainctx:
            tpool = mainctx.enter_context(tc.tile_pool(name="tpool", bufs=TB))
            epool = mainctx.enter_context(tc.tile_pool(name="epool", bufs=EB))
            accp = mainctx.enter_context(tc.tile_pool(name="accp", bufs=3))
            endp = mainctx.enter_context(tc.tile_pool(name="endp", bufs=1))

            prog, rows, banks, groups = build_program()
            last_fin = {}
            row_of = {}
            for rid in range(len(rows)):
                row_of[(rows[rid][2], rows[rid][3])] = rid
            for index in range(len(prog)):
                if prog[index][0] == "fin":
                    rid = row_of[(prog[index][1], prog[index][2])]
                    last_fin[(rows[rid][1] + 1) % 2] = index
                    last_fin[2] = index
            bank_count = {"A": 0, "B": 0}
            bank_tag = []
            for kind, size in banks:
                bank_tag.append("b%d" % ((0 if kind == "A" else 2) + bank_count[kind] % 2))
                bank_count[kind] += 1

            s1c = [endp.tile([P, NX + 2], F32, name="s1c%d" % i) for i in range(2)]
            s2c = endp.tile([P, N], F32, name="s2c")
            terms = {}
            lts = {}
            ets = {}
            accs = {}
            es = {}
            idles = []
            with tc.manual_schedule(engines=pinned):
                s1 = [psum.tile([P, 512], F32, name="s1", tag="b%d" % (4 + i)) for i in range(2)]
                s2 = psum.tile([P, 512], F32, name="s2", tag="b6")
                for acc0, width in ((s1[0], 512), (s1[1], 512), (s2, 512)):
                    for c in range(width // P):
                        nc.tensor.matmul(out=acc0[:, c * P:(c + 1) * P], lhsT=zero[:], rhs=ident[:], is_transpose=True, start=(c == 0), stop=False)

                for piece in range(XH1 + XH2):
                    if piece % XP == XP - 1:
                        xstore(piece // (2 * XP), (piece % (2 * XP)) // XP)
                hold = psum.tile([P, 512], F32, name="hold", tag="b3")
                for i in range(HOLD):
                    nc.tensor.matmul_mx(out=hold[:], lhsT=xq[:, 0:P].bitcast(FP8X4), lhsT_scale=xsc[:, 0:P],
                                        rhs=tq0[:, 0:512].bitcast(FP8X4), rhs_scale=tsc0[:, 0:512], start=True, stop=True)

                for index in range(len(prog)):
                    item = prog[index]
                    what = item[0]
                    if what == "abs" or what == "ts":
                        rid, k = item[1], item[2]
                        n = rows[rid][1]
                        if k == 0:
                            a = tpool.tile([P, K, P], F32, name="a", tag="a")
                            terms[rid] = a
                        if what == "abs":
                            nc.scalar.activation(out=terms[rid][:, k, :], in_=fsx[:, k, n + 1:n + 1 + P], func=ACT.Abs, scale=-1.0,
                                                 bias=fsx[:, k, n:n + 1])
                        elif k == K - 1 and not rows[rid][4]:
                            nc.vector.scalar_tensor_tensor(out=terms[rid][:, k, :], in0=fsx[:, k, n + 1:n + 1 + P], scalar=fsx[:, k, n:n + 1],
                                                           in1=snegx[:, n + 1:n + 1 + P], op0=ALU.max, op1=ALU.add)
                        elif k == K - 2:
                            nc.vector.tensor_scalar(out=terms[rid][:, k, :], in0=fsx[:, k, n + 1:n + 1 + P], scalar1=fsx[:, k, n:n + 1],
                                                    scalar2=snegx[:, n:n + 1], op0=ALU.max, op1=ALU.add)
                        else:
                            nc.vector.tensor_scalar(out=terms[rid][:, k, :], in0=fsx[:, k, n + 1:n + 1 + P], scalar1=fsx[:, k, n:n + 1],
                                                    scalar2=None, op0=ALU.max)
                    elif what == "tp":
                        rid, k = item[1], item[2]
                        kind, n, bank, q, opened = rows[rid]
                        first = (k == 0)
                        if first and q == 0:
                            lt = psum.tile([P, RB, P], F32, name="lt", tag=bank_tag[bank])
                            lts[bank] = lt
                        nc.tensor.matmul(out=lts[bank][:, q, :], lhsT=(snegx[:, n + 1:n + 1 + P] if k == K else terms[rid][:, k, :]), rhs=ident[:],
                                         is_transpose=True, start=first, stop=(k == (K if opened else K - 1)))
                    elif what == "bexp":
                        bank = item[1]
                        kind, size = banks[bank]
                        et = epool.tile([P, RB, P], F32, name="et", tag="et")
                        ets[bank] = et
                        nc.scalar.activation(out=et[:, 0:size, :], in_=lts[bank][:, 0:size, :], func=ACT.Exp, scale=(-1.0 if kind == "A" else -2.0))
                    elif what == "fin":
                        bank, q = item[1], item[2]
                        n = rows[row_of[(bank, q)]][1]
                        par = (n + 1) % 2
                        nc.tensor.matmul(out=s2[:, n:n + ROWN], lhsT=ets[bank][:, q, :], rhs=onesz[:], start=False, stop=(last_fin[2] == index))
                        nc.tensor.matmul(out=s1[par][:, n + 1 + par:n + 1 + par + P], lhsT=ets[bank][:, q, :], rhs=ident[:], is_transpose=True,
                                         start=False, stop=(last_fin[par] == index))
                        if last_fin[par] == index:
                            nc.vector.tensor_copy(out=s1c[par][:], in_=s1[par][:, 0:NX + 2])
                        if last_fin[2] == index:
                            nc.scalar.copy(out=s2c[:], in_=s2[:, 0:N])
                    elif what == "warm":
                        if len(idles) == 0:
                            idle = psum.tile([P, 512], F32, name="idle", tag="b7")
                            idles.append(idle)
                        nc.tensor.matmul_mx(out=idles[0][:], lhsT=xq[:, 0:P].bitcast(FP8X4), lhsT_scale=xsc[:, 0:P],
                                            rhs=tq0[:, 0:512].bitcast(FP8X4), rhs_scale=tsc0[:, 0:512], start=True, stop=True)
                    elif what == "stt":
                        g, k, r = item[1], item[2], item[3]
                        n = groups[g] + r
                        if k == 0 and r == 0:
                            acc = accp.tile([P, RV, P], F32, name="acc", tag="acc")
                            accs[g] = acc
                        nc.vector.scalar_tensor_tensor(
                            out=accs[g][:, r, :],
                            in0=fsx[:, k, n + 1:n + 1 + P],
                            scalar=fsx[:, k, n:n + 1],
                            in1=(snegx[:, n + 1:n + 1 + P] if k == 0 else accs[g][:, r, :]),
                            op0=ALU.max,
                            op1=ALU.add,
                        )
                    elif what == "cexp":
                        g, r = item[1], item[2]
                        n = groups[g] + r
                        if r == 0:
                            e = accp.tile([P, RV, P], F32, name="e", tag="e")
                            es[g] = e
                        nc.scalar.activation(out=es[g][:, r, :], in_=accs[g][:, r, :], func=ACT.Exp, scale=-2.0,
                                             bias=ssum[:, n:n + 1], accum_out=rowsum[:, n:n + 1])
                    elif what == "cadd":
                        g, i = item[1], item[2]
                        n0 = groups[g]
                        if i == 0:
                            nc.vector.tensor_tensor(out=rowsum[:, n0:n0 + RV], in0=rowsum[:, n0:n0 + RV], in1=es[g][:, :, P - 1], op=ALU.subtract)
                        else:
                            n = n0 + i - 1
                            nc.vector.tensor_tensor(out=colx[:, n + 1:n + 1 + P], in0=colx[:, n + 1:n + 1 + P], in1=es[g][:, i - 1, :], op=ALU.add)
                    elif what == "wrap":
                        i = item[1]
                        if i < K // 2:
                            nc.vector.tensor_copy(out=fsx[:, 2 * i:2 * i + 2, N:NX], in_=fsx[:, 2 * i:2 * i + 2, 0:P])
                        else:
                            nc.vector.tensor_copy(out=snegx[:, N:NX], in_=snegx[:, 0:P])
                    elif what == "sneg":
                        nc.vector.tensor_scalar(out=snegx[:, 0:N], in0=sp[:], scalar1=-0.5, scalar2=None, op0=ALU.mult)
                    elif what == "ssum":
                        nc.scalar.copy(out=ssum[:], in_=sp[:])
                    else:
                        assert what == "xout"
                        xout(item[1], item[2], True)

                late = (rows[row_of[(prog[last_fin[2]][1], prog[last_fin[2]][2])]][1] + 1) % 2
                pts = [psum.tile([P, J], F32, name="pt", tag="b%d" % t) for t in range(2)]
                parts = [[], []]
                for t in range(2):
                    parts[t] = [rowsum[:, t * P:(t + 1) * P], colx[:, t * P:(t + 1) * P]]
                parts[0].append(colx[:, N:NX])
                early_count = [len(parts[0]), len(parts[1])]
                for par in (1 - late, late):
                    for t in range(2):
                        parts[t].append(s1c[par][:, t * P + par:(t + 1) * P + par])
                    parts[0].append(s1c[par][:, N + par:NX + par])
                for t in range(2):
                    parts[t].append(s2c[:, t * P:(t + 1) * P])
                for t in range(2):
                    for i in range(early_count[t]):
                        nc.tensor.matmul(out=pts[t][:], lhsT=parts[t][i], rhs=ident[:], is_transpose=True, start=(i == 0), stop=False)
                o0 = endp.tile([P, 2, J], F32, name="o0")
                o8 = [endp.tile([P, J], FP8, name="o8%d" % t) for t in range(2)]
                for t in range(2):
                    for i in range(early_count[t], len(parts[t])):
                        nc.tensor.matmul(out=pts[t][:], lhsT=parts[t][i], rhs=ident[:], is_transpose=True, start=False, stop=(i == len(parts[t]) - 1))
                    if t == 0:
                        nc.vector.tensor_copy(out=o0[:, t, :], in_=pts[t][:])
                        nc.vector.tensor_scalar(out=o8[t][:], in0=pts[t][:], scalar1=Y_SCALE, scalar2=None, op0=ALU.mult, saturate=False)
                    else:
                        nc.scalar.copy(out=o0[:, t, :], in_=pts[t][:])
                        nc.scalar.activation(out=o8[t][:], in_=pts[t][:], func=ACT.Copy, scale=Y_SCALE, saturate=False)
                    nc.sync.dma_start(out=out_0[t * P:(t + 1) * P, IN_F:IN_F + J], in_=o0[:, t, :])
                    nc.sync.dma_start(out=out_1[t * P:(t + 1) * P, IN_F:IN_F + J], in_=o8[t][:].bitcast(U8))
